import numpy as np
import ml_dtypes


def mxq(x, axis, fmt="e4m3"):
    dtype, down = {"e4m3": (ml_dtypes.float8_e4m3fn, 7), "e5m2": (ml_dtypes.float8_e5m2, 14)}[fmt]
    v = np.moveaxis(np.asarray(x, np.float32).astype(ml_dtypes.bfloat16).astype(np.float64), axis, -1)
    blocks = v.reshape(v.shape[:-1] + (-1, 32))
    amax = np.abs(blocks).max(-1, keepdims=True)
    byte = np.maximum(np.where(amax > 0, np.frexp(amax)[1] - 1 + 127, 0) - down, 1)
    scale = np.exp2(byte - 127.0)
    codes = (blocks / scale).astype(np.float32).astype(dtype).astype(np.float64)
    return np.moveaxis((codes * scale).reshape(v.shape), -1, axis)


WIDE = False


def mx_kscale(k):
    if not WIDE:
        return np.ones(k)
    levels = np.array([10, -10, 5, -5, 0])
    if k % 512:
        return np.exp2(np.random.permutation(np.resize(levels, k // 32))).repeat(32)
    a = np.empty((k // 512, 16))
    for p in range(k // 512):
        a[p, :8] = np.random.permutation(np.resize(levels, 8))
        for g in range(8):
            far = levels[np.abs(levels - a[p, g]) >= 10]
            a[p, g + 8] = far[np.random.randint(len(far))]
    return np.exp2(a.ravel()).repeat(32)


BF16 = ml_dtypes.bfloat16


def bf(x):
    return np.asarray(x, np.float32).astype(BF16)


def f64(x):
    return np.asarray(x).astype(np.float64)


B, T, D, H = 8, 512, 1024, 384


def sigmoid(v):
    return 1.0 / (1.0 + np.exp(-v))


def setup_inputs():
    s = mx_kscale(D)
    return {"x": bf(np.random.standard_normal((B, T, D)) * s),
            "Wq": bf(np.random.standard_normal((H, D)) * 1.0 / np.sqrt(D) / s),
            "bq": bf(np.random.standard_normal(H) * 0.5),
            "Wk": bf(np.random.standard_normal((H, D)) * 0.6 / np.sqrt(D) / s),
            "bk": bf(np.random.standard_normal(H) * 0.3),
            "Wv": bf(np.random.standard_normal((H, D)) * 2.0 / np.sqrt(D) / s),
            "bv": bf(np.random.standard_normal(H) * 0.5),
            "wbias": bf(np.random.uniform(0.0, 1.0, H))}


def reference(x, Wq, bq, Wk, bk, Wv, bv, wbias):
    xq = mxq(f64(x), 2, "e4m3")
    Q = (xq @ mxq(f64(Wq), 1, "e4m3").T) + f64(bq)
    K = (xq @ mxq(f64(Wk), 1, "e4m3").T) + f64(bk)
    V = (xq @ mxq(f64(Wv), 1, "e4m3").T) + f64(bv)
    Q_sig = sigmoid(Q)
    numer = np.exp(K + f64(wbias))
    denom = numer.sum(axis=0)
    weighted = (numer * V).sum(axis=0) / denom
    Yt = Q_sig * weighted
    return Yt

@@ -1,0 +1,325 @@
+from contextlib import ExitStack
+
+import concourse.masks as masks
+import concourse.mybir as mybir
+
+F32 = mybir.dt.float32
+BF16 = mybir.dt.bfloat16
+U32 = mybir.dt.uint32
+U8 = mybir.dt.uint8
+FP8X4 = mybir.dt.float8_e4m3fn_x4
+ACT = mybir.ActivationFunctionType
+ALU = mybir.AluOpType
+
+B, T, DM, H = 8, 512, 1024, 384
+P = 128
+J = T // P
+HB = H // P
+PAIRS = 2 * B
+FLOPS = 2 * B * T * DM * 3 * H
+
+MK, MV, MQ = 0, 1, 2
+
+K_FIRST = 3
+EARLY = B - K_FIRST
+
+Q_AFTER_EARLY = (0, 0, 0, 2, 2)
+Q_AFTER_LATE_K = (1, 2, 4)
+Q_AFTER_LATE_V = 2
+Q_IN_MEAN = (2, 1)
+
+TANH_AHEAD = 6
+TANH_BEFORE_MEAN = 3
+
+X_BUFS = 4
+
+
+def tile_aftattention_t_kernel(tc, x, Wq, bq, Wk, bk, Wv, bv, wbias, out):
+    nc = tc.nc
+    with ExitStack() as ctx:
+        keep = ctx.enter_context(tc.tile_pool(name="keep", bufs=1))
+        stage = ctx.enter_context(tc.tile_pool(name="stage", bufs=2))
+        psum = ctx.enter_context(tc.psum_pool(name="psum", bufs=8))
+
+        def bank():
+            return psum.tile([P, 512], F32, name="ps", tag="ps", bufs=8)
+
+        ident = keep.tile([P, P], F32, name="ident")
+        masks.make_identity(nc, ident[:])
+
+        w_codes = keep.tile([P, 3, 2 * H], U32, name="w_codes", align_bytes=64)
+        w_sc = keep.tile([P, 3, 2 * H], U8, name="w_sc", align_bytes=64)
+        x_codes = keep.tile([P, B, 2, T], U32, name="x_codes", align_bytes=64)
+        x_sc = keep.tile([P, B, 2, T], U8, name="x_sc", align_bytes=64)
+        d_sum = keep.tile([P, HB, T], F32, name="d_sum")
+        n_sum = keep.tile([P, HB, T], F32, name="n_sum")
+        hw = keep.tile([P, J, H], F32, name="hw")
+        th = keep.tile([P, B, HB, T], F32, name="th")
+        b_rows = keep.tile([P, P], BF16, name="b_rows")
+        b_rows32 = keep.tile([P, P], F32, name="b_rows32")
+        b_cols = keep.tile([P, 8], F32, name="b_cols")
+        warm = keep.tile([P, 1], F32, name="warm")
+
+        w_dram = (Wk, Wv, Wq)
+        w_raw = {}
+        w_grp = {}
+        x_tiles = {}
+        grp_tiles = {}
+        quantised = []
+        e_tiles = {}
+        p_tiles = {}
+        o_tiles = {}
+        tanh_banks = {}
+
+        def load_w(m):
+            w_raw[m] = stage.tile([P, HB, DM], BF16, name="w_raw", tag="six", bufs=5, align_bytes=64)
+            for r in range(HB):
+                nc.sync.dma_start(out=w_raw[m][:, r, :], in_=w_dram[m][r * P : (r + 1) * P, :])
+
+        def load_x(b, parts):
+            x_tiles[b] = stage.tile([P, J, DM], BF16, name="x_raw", tag="x_raw", bufs=X_BUFS)
+            src = x[b].rearrange("(p j) k -> p j k", j=J)
+            step = J // parts
+            for i in range(parts):
+                nc.sync.dma_start(
+                    out=x_tiles[b][:, i * step : (i + 1) * step, :], in_=src[:, i * step : (i + 1) * step, :]
+                )
+
+        def transpose_words(dst_bank, src_bf16):
+            words = src_bf16.bitcast(F32)
+            for c in range(4):
+                g, u = c // 2, c % 2
+                nc.tensor.transpose(
+                    dst_bank[:, c * P : (c + 1) * P], words[:, 256 * g + u : 256 * (g + 1) : 2], ident[:]
+                )
+
+        def grouped(ps):
+            return ps[:].rearrange("p (g u r) -> p g r u", g=2, u=2)
+
+        def transpose_w(m, r, engine):
+            if r == 0:
+                w_grp[m] = stage.tile([P, 2 * H * 4], BF16, name="w_grp", tag="six", bufs=5, align_bytes=64)
+            grp32 = w_grp[m][:].bitcast(F32).rearrange("p (g h u) -> p g h u", g=2, u=2)
+            ps = bank()
+            transpose_words(ps, w_raw[m][:, r, :])
+            dst = grp32[:, :, r * P : (r + 1) * P, :]
+            if engine == "s":
+                nc.scalar.copy(out=dst, in_=grouped(ps))
+            else:
+                nc.vector.tensor_copy(out=dst, in_=grouped(ps))
+
+        def quantise_w(m, r):
+            for g in range(2):
+                cols = slice(g * H + r * P, g * H + (r + 1) * P)
+                nc.vector.quantize_mx(
+                    out=w_codes[:, m, cols].bitcast(FP8X4),
+                    scales=w_sc[:, m, cols],
+                    in_=w_grp[m][:, 4 * (g * H + r * P) : 4 * (g * H + (r + 1) * P)],
+                )
+
+        def transpose_x_upto(n):
+            while len(grp_tiles) < n:
+                q = len(grp_tiles)
+                b, half = q // 2, q % 2
+                grp = stage.tile([P, 2048], BF16, name="x_grp", tag="x_grp", bufs=3, align_bytes=64)
+                grp_tiles[q] = grp
+                grp32 = grp[:].bitcast(F32).rearrange("p (g r u) -> p g r u", g=2, u=2)
+                for s in range(2):
+                    ps = bank()
+                    transpose_words(ps, x_tiles[b][:, 2 * half + s, :])
+                    nc.scalar.copy(out=grp32[:, :, s * P : (s + 1) * P, :], in_=grouped(ps))
+                if half == 1 and b + X_BUFS < B:
+                    load_x(b + X_BUFS, 1)
+
+        def quantise_x_upto(n):
+            while len(quantised) < n:
+                q = len(quantised)
+                quantised.append(q)
+                b, half = q // 2, q % 2
+                for g in range(2):
+                    nc.vector.quantize_mx(
+                        out=x_codes[:, b, g, half * 256 : (half + 1) * 256].bitcast(FP8X4),
+                        scales=x_sc[:, b, g, half * 256 : (half + 1) * 256],
+                        in_=grp_tiles[q][:, g * 1024 : (g + 1) * 1024],
+                    )
+
+        def project(m, b, hb):
+            ps = bank()
+            for g in range(2):
+                cols = slice(g * H + hb * P, g * H + (hb + 1) * P)
+                nc.tensor.matmul_mx(
+                    out=ps[:],
+                    lhsT=w_codes[:, m, cols].bitcast(FP8X4),
+                    lhsT_scale=w_sc[:, m, cols],
+                    rhs=x_codes[:, b, g, :].bitcast(FP8X4),
+                    rhs_scale=x_sc[:, b, g, :],
+                    start=(g == 0),
+                    stop=(g == 1),
+                )
+            return ps
+
+        def k_units(b):
+            e_tiles[b] = stage.tile([P, HB, T], F32, name="e_t", tag="e_t", bufs=K_FIRST + 1)
+            for hb in range(HB):
+                ps = project(MK, b, hb)
+                nc.scalar.activation(out=e_tiles[b][:, hb, :], in_=ps[:], func=ACT.Exp)
+
+        def v_units(b):
+            if b > 0:
+                p_tiles[b] = stage.tile([P, HB, T], F32, name="p_t", tag="six", bufs=5, align_bytes=64)
+            for hb in range(HB):
+                ps = project(MV, b, hb)
+                nc.vector.scalar_tensor_tensor(
+                    out=n_sum[:, hb, :] if b == 0 else p_tiles[b][:, hb, :],
+                    in0=ps[:],
+                    scalar=b_cols[:, HB + hb : HB + hb + 1],
+                    in1=e_tiles[b][:, hb, :],
+                    op0=ALU.add,
+                    op1=ALU.mult,
+                )
+
+        q_order = [(b, hb) for b in range(B) for hb in range(HB)]
+        q_issued = []
+
+        def q_units(n):
+            for b, hb in q_order[len(q_issued) : len(q_issued) + n]:
+                assert 2 * b + 2 <= len(quantised)
+                q_issued.append((b, hb))
+                ps = project(MQ, b, hb)
+                nc.scalar.activation(
+                    out=th[:, b, hb, :], in_=ps[:], func=ACT.Tanh, bias=b_cols[:, hb : hb + 1], scale=0.5
+                )
+
+        def add_exponentials(b):
+            if b >= 1:
+                first = e_tiles[0][:] if b == 1 else d_sum[:]
+                nc.vector.tensor_tensor(out=d_sum[:], in0=first, in1=e_tiles[b][:], op=ALU.add)
+
+        def add_products(b, hbs):
+            if b >= 1:
+                nc.vector.tensor_tensor(
+                    out=n_sum[:, hbs, :], in0=n_sum[:, hbs, :], in1=p_tiles[b][:, hbs, :], op=ALU.add
+                )
+
+        def tokens_to_partitions(src):
+            ps = bank()
+            for j in range(J):
+                nc.tensor.transpose(ps[:, j * P : (j + 1) * P], src[:, j * P : (j + 1) * P], ident[:])
+            return ps
+
+        def weighted_mean(hb):
+            nc.vector.tensor_tensor(out=n_sum[:, hb, :], in0=n_sum[:, hb, :], in1=d_sum[:, hb, :], op=ALU.mult)
+            q_units(Q_IN_MEAN[0])
+            ps = tokens_to_partitions(n_sum[:, hb, :])
+            q_units(Q_IN_MEAN[1])
+            nc.scalar.mul(
+                out=hw[:, :, hb * P : (hb + 1) * P], in_=ps[:].rearrange("p (j h) -> p j h", j=J), mul=0.5
+            )
+
+        def transpose_tanh(b, hb):
+            tanh_banks[(b, hb)] = tokens_to_partitions(th[:, b, hb, :])
+
+        def finish(b, hb):
+            if b not in o_tiles:
+                o_tiles[b] = stage.tile([P, J, H], F32, name="o_sb", tag="x_raw", bufs=X_BUFS)
+            cols = slice(hb * P, (hb + 1) * P)
+            nc.vector.scalar_tensor_tensor(
+                out=o_tiles[b][:, :, cols],
+                in0=tanh_banks[(b, hb)][:].rearrange("p (j h) -> p j h", j=J),
+                scalar=1.0,
+                in1=hw[:, :, cols],
+                op0=ALU.add,
+                op1=ALU.mult,
+            )
+            dst = out[b].rearrange("(p j) h -> p j h", j=J)
+            if b == B - 1:
+                nc.sync.dma_start(out=dst[:, :, cols], in_=o_tiles[b][:, :, cols])
+            elif hb == HB - 1:
+                nc.sync.dma_start(out=dst, in_=o_tiles[b][:])
+
+        nc.vector.memset(b_rows[:], 0.0)
+        nc.scalar.dma_start(out=b_rows[0:HB, :], in_=bq.rearrange("(r c) -> r c", c=P))
+        nc.scalar.dma_start(out=b_rows[HB : 2 * HB, :], in_=bv.rearrange("(r c) -> r c", c=P))
+        nc.vector.memset(warm[:], 0.0)
+        nc.scalar.activation(out=warm[:], in_=warm[:], func=ACT.Exp)
+
+        load_x(0, 2)
+        load_w(MK)
+        load_w(MV)
+        load_x(1, 2)
+        load_x(2, 2)
+        load_x(3, 1)
+
+        transpose_x_upto(2)
+        load_w(MQ)
+        quantise_x_upto(1)
+        transpose_w(MK, 0, "v")
+        quantise_w(MK, 0)
+        quantise_x_upto(2)
+        transpose_w(MK, 1, "v")
+        transpose_w(MK, 2, "s")
+        quantise_w(MK, 1)
+        quantise_w(MK, 2)
+        transpose_w(MV, 0, "s")
+        nc.vector.tensor_copy(out=b_rows32[:], in_=b_rows[:])
+        quantise_w(MV, 0)
+        k_units(0)
+        transpose_w(MV, 1, "v")
+        transpose_w(MV, 2, "s")
+        ps_b = bank()
+        nc.tensor.transpose(ps_b[:, 0:P], b_rows32[:], ident[:])
+        transpose_x_upto(4)
+        quantise_w(MV, 1)
+        quantise_w(MV, 2)
+        nc.vector.tensor_scalar_mul(out=b_cols[:, 0:HB], in0=ps_b[:, 0:HB], scalar1=0.5)
+        nc.vector.tensor_copy(out=b_cols[:, HB : 2 * HB], in_=ps_b[:, HB : 2 * HB])
+        quantise_x_upto(4)
+        v_units(0)
+        q_units(Q_AFTER_EARLY[0])
+
+        for b in range(1, EARLY):
+            transpose_x_upto(3 * b + 2)
+            k_units(b)
+            if b == 2:
+                for r in range(HB):
+                    transpose_w(MQ, r, "s")
+            add_products(b - 1, slice(0, HB))
+            quantise_x_upto(3 * b + 2)
+            transpose_x_upto(3 * b + 4)
+            add_exponentials(b)
+            v_units(b)
+            quantise_x_upto(3 * b + 3)
+            if b == 2:
+                for r in range(HB):
+                    quantise_w(MQ, r)
+            q_units(Q_AFTER_EARLY[b])
+        add_products(EARLY - 1, slice(0, HB))
+        quantise_x_upto(PAIRS)
+
+        for b in range(EARLY, B):
+            k_units(b)
+            add_exponentials(b)
+            q_units(Q_AFTER_LATE_K[b - EARLY])
+        for hb in range(HB):
+            nc.scalar.activation(out=d_sum[:, hb, :], in_=d_sum[:, hb, :], func=ACT.Ln)
+        for hb in range(HB):
+            nc.scalar.activation(out=d_sum[:, hb, :], in_=d_sum[:, hb, :], func=ACT.Exp, scale=-1.0)
+        for b in range(EARLY, B):
+            v_units(b)
+        q_units(Q_AFTER_LATE_V)
+
+        last = [(2 * bb + b, hb) for bb in range(B // 2) for hb in range(HB) for b in range(2)]
+        for b, hb in last[:TANH_BEFORE_MEAN]:
+            transpose_tanh(b, hb)
+        for hb in range(HB):
+            for b in range(EARLY, B):
+                add_products(b, slice(hb, hb + 1))
+            weighted_mean(hb)
+        for b, hb in last[TANH_BEFORE_MEAN:TANH_AHEAD]:
+            transpose_tanh(b, hb)
+        for n in range(len(last)):
+            finish(last[n][0], last[n][1])
+            if n == 0:
+                q_units(len(q_order))
+            if n + TANH_AHEAD < len(last):
+                transpose_tanh(last[n + TANH_AHEAD][0], last[n + TANH_AHEAD][1])

@@ -14,24 +14,17 @@ ALU = mybir.AluOpType
 B, T, DM, H = 8, 512, 1024, 384
 P = 128
 J = T // P
+JH = J // 2
 HB = H // P
-PAIRS = 2 * B
+PAIRS = B // 2
+N = 512
+HALF = N // 2
 FLOPS = 2 * B * T * DM * 3 * H
 
 MK, MV, MQ = 0, 1, 2
-
-K_FIRST = 3
-EARLY = B - K_FIRST
-
-Q_AFTER_EARLY = (0, 0, 0, 2, 2)
-Q_AFTER_LATE_K = (1, 2, 4)
-Q_AFTER_LATE_V = 2
-Q_IN_MEAN = (2, 1)
-
-TANH_AHEAD = 6
-TANH_BEFORE_MEAN = 3
-
-X_BUFS = 4
+PERM = ()
+S_PERM = ()
+G_ADD = ()
 
 
 def tile_aftattention_t_kernel(tc, x, Wq, bq, Wk, bk, Wv, bv, wbias, out):
@@ -40,21 +33,18 @@ def tile_aftattention_t_kernel(tc, x, Wq, bq, Wk, bk, Wv, bv, wbias, out):
         keep = ctx.enter_context(tc.tile_pool(name="keep", bufs=1))
         stage = ctx.enter_context(tc.tile_pool(name="stage", bufs=2))
         psum = ctx.enter_context(tc.psum_pool(name="psum", bufs=8))
+        ctx.enter_context(tc.manual_schedule())
 
         def bank():
-            return psum.tile([P, 512], F32, name="ps", tag="ps", bufs=8)
+            return psum.tile([P, N], F32, name="ps", tag="ps", bufs=8)
 
         ident = keep.tile([P, P], F32, name="ident")
         masks.make_identity(nc, ident[:])
 
         w_codes = keep.tile([P, 3, 2 * H], U32, name="w_codes", align_bytes=64)
         w_sc = keep.tile([P, 3, 2 * H], U8, name="w_sc", align_bytes=64)
-        x_codes = keep.tile([P, B, 2, T], U32, name="x_codes", align_bytes=64)
-        x_sc = keep.tile([P, B, 2, T], U8, name="x_sc", align_bytes=64)
-        d_sum = keep.tile([P, HB, T], F32, name="d_sum")
-        n_sum = keep.tile([P, HB, T], F32, name="n_sum")
-        hw = keep.tile([P, J, H], F32, name="hw")
-        th = keep.tile([P, B, HB, T], F32, name="th")
+        x_codes = keep.tile([P, 2, 2, B * HALF], U32, name="x_codes", align_bytes=64)
+        x_sc = keep.tile([P, 2, 2, B * HALF], U8, name="x_sc", align_bytes=64)
         b_rows = keep.tile([P, P], BF16, name="b_rows")
         b_rows32 = keep.tile([P, P], F32, name="b_rows32")
         b_cols = keep.tile([P, 8], F32, name="b_cols")
@@ -63,12 +53,15 @@ def tile_aftattention_t_kernel(tc, x, Wq, bq, Wk, bk, Wv, bv, wbias, out):
         w_dram = (Wk, Wv, Wq)
         w_raw = {}
         w_grp = {}
-        x_tiles = {}
-        grp_tiles = {}
-        quantised = []
+        x_raw = {}
+        x_perm = {}
+        x_grp = {}
         e_tiles = {}
         p_tiles = {}
-        o_tiles = {}
+        d_sum = {}
+        n_sum = {}
+        hw = {}
+        th_tiles = {}
         tanh_banks = {}
 
         def load_w(m):
@@ -76,37 +69,42 @@ def tile_aftattention_t_kernel(tc, x, Wq, bq, Wk, bk, Wv, bv, wbias, out):
             for r in range(HB):
                 nc.sync.dma_start(out=w_raw[m][:, r, :], in_=w_dram[m][r * P : (r + 1) * P, :])
 
-        def load_x(b, parts):
-            x_tiles[b] = stage.tile([P, J, DM], BF16, name="x_raw", tag="x_raw", bufs=X_BUFS)
-            src = x[b].rearrange("(p j) k -> p j k", j=J)
-            step = J // parts
-            for i in range(parts):
-                nc.sync.dma_start(
-                    out=x_tiles[b][:, i * step : (i + 1) * step, :], in_=src[:, i * step : (i + 1) * step, :]
+        def load_x(s, i, parts):
+            x_raw[(s, i)] = stage.tile([P, 2, JH, DM], BF16, name="x_raw", tag="x_raw", bufs=4)
+            for k in range(2):
+                src = x[2 * i + k].rearrange("(p j) k -> p j k", j=J)[:, JH * s : JH * (s + 1), :]
+                for c in range(parts):
+                    js = slice(c * JH // parts, (c + 1) * JH // parts)
+                    nc.sync.dma_start(out=x_raw[(s, i)][:, k, js, :], in_=src[:, js, :])
+
+        def permute_x(s, i):
+            for k in range(2):
+                x_perm[(s, i, k)] = stage.tile([P, JH * DM // 2], F32, name="x_perm", tag="x_perm", bufs=3)
+                (nc.scalar.copy if (s, i) in S_PERM else nc.vector.tensor_copy)(
+                    out=x_perm[(s, i, k)][:].rearrange("p (jg u w) -> p jg u w", jg=2 * JH, u=2),
+                    in_=x_raw[(s, i)][:, k, :, :]
+                    .rearrange("p j k -> p (j k)")
+                    .bitcast(F32)
+                    .rearrange("p (jg w u) -> p jg u w", jg=2 * JH, u=2),
                 )
 
-        def transpose_words(dst_bank, src_bf16):
-            words = src_bf16.bitcast(F32)
+        def transpose_words(dst_bank, words, permuted):
             for c in range(4):
                 g, u = c // 2, c % 2
-                nc.tensor.transpose(
-                    dst_bank[:, c * P : (c + 1) * P], words[:, 256 * g + u : 256 * (g + 1) : 2], ident[:]
-                )
+                src = words[:, c * P : (c + 1) * P] if permuted else words[:, 256 * g + u : 256 * (g + 1) : 2]
+                nc.tensor.transpose(dst_bank[:, c * P : (c + 1) * P], src, ident[:])
 
-        def grouped(ps):
-            return ps[:].rearrange("p (g u r) -> p g r u", g=2, u=2)
+        def copy_grouped(engine, dst, ps):
+            copy = nc.scalar.copy if engine == "s" else nc.vector.tensor_copy
+            copy(out=dst, in_=ps[:].rearrange("p (g u r) -> p g r u", g=2, u=2))
 
         def transpose_w(m, r, engine):
             if r == 0:
                 w_grp[m] = stage.tile([P, 2 * H * 4], BF16, name="w_grp", tag="six", bufs=5, align_bytes=64)
             grp32 = w_grp[m][:].bitcast(F32).rearrange("p (g h u) -> p g h u", g=2, u=2)
             ps = bank()
-            transpose_words(ps, w_raw[m][:, r, :])
-            dst = grp32[:, :, r * P : (r + 1) * P, :]
-            if engine == "s":
-                nc.scalar.copy(out=dst, in_=grouped(ps))
-            else:
-                nc.vector.tensor_copy(out=dst, in_=grouped(ps))
+            transpose_words(ps, w_raw[m][:, r, :].bitcast(F32), False)
+            copy_grouped(engine, grp32[:, :, r * P : (r + 1) * P, :], ps)
 
         def quantise_w(m, r):
             for g in range(2):
@@ -117,125 +115,143 @@ def tile_aftattention_t_kernel(tc, x, Wq, bq, Wk, bk, Wv, bv, wbias, out):
                     in_=w_grp[m][:, 4 * (g * H + r * P) : 4 * (g * H + (r + 1) * P)],
                 )
 
-        def transpose_x_upto(n):
-            while len(grp_tiles) < n:
-                q = len(grp_tiles)
-                b, half = q // 2, q % 2
-                grp = stage.tile([P, 2048], BF16, name="x_grp", tag="x_grp", bufs=3, align_bytes=64)
-                grp_tiles[q] = grp
-                grp32 = grp[:].bitcast(F32).rearrange("p (g r u) -> p g r u", g=2, u=2)
-                for s in range(2):
-                    ps = bank()
-                    transpose_words(ps, x_tiles[b][:, 2 * half + s, :])
-                    nc.scalar.copy(out=grp32[:, :, s * P : (s + 1) * P, :], in_=grouped(ps))
-                if half == 1 and b + X_BUFS < B:
-                    load_x(b + X_BUFS, 1)
+        def transpose_x(s, i, engines="ssss"):
+            x_grp[(s, i)] = stage.tile([P, 2 * N * 4], BF16, name="x_grp", tag="x_grp", bufs=2, align_bytes=64)
+            grp32 = x_grp[(s, i)][:].bitcast(F32).rearrange("p (g c u) -> p g c u", g=2, u=2)
+            for c in range(2 * JH):
+                ps = bank()
+                if (s, i, 0) in x_perm:
+                    transpose_words(ps, x_perm[(s, i, c // JH)][:, (c % JH) * 512 : (c % JH + 1) * 512], True)
+                else:
+                    transpose_words(ps, x_raw[(s, i)][:, c // JH, c % JH, :].bitcast(F32), False)
+                copy_grouped(engines[c], grp32[:, :, c * P : (c + 1) * P, :], ps)
 
-        def quantise_x_upto(n):
-            while len(quantised) < n:
-                q = len(quantised)
-                quantised.append(q)
-                b, half = q // 2, q % 2
+        def quantise_x(s, i, parts=1):
+            for c in range(parts):
+                w = N // parts
                 for g in range(2):
+                    cols = slice(i * N + c * w, i * N + (c + 1) * w)
                     nc.vector.quantize_mx(
-                        out=x_codes[:, b, g, half * 256 : (half + 1) * 256].bitcast(FP8X4),
-                        scales=x_sc[:, b, g, half * 256 : (half + 1) * 256],
-                        in_=grp_tiles[q][:, g * 1024 : (g + 1) * 1024],
+                        out=x_codes[:, s, g, cols].bitcast(FP8X4),
+                        scales=x_sc[:, s, g, cols],
+                        in_=x_grp[(s, i)][:, 4 * (g * N + c * w) : 4 * (g * N + (c + 1) * w)],
                     )
 
-        def project(m, b, hb):
+        def project(m, s, i, hb):
             ps = bank()
             for g in range(2):
                 cols = slice(g * H + hb * P, g * H + (hb + 1) * P)
+                toks = slice(i * N, (i + 1) * N)
                 nc.tensor.matmul_mx(
                     out=ps[:],
                     lhsT=w_codes[:, m, cols].bitcast(FP8X4),
                     lhsT_scale=w_sc[:, m, cols],
-                    rhs=x_codes[:, b, g, :].bitcast(FP8X4),
-                    rhs_scale=x_sc[:, b, g, :],
+                    rhs=x_codes[:, s, g, toks].bitcast(FP8X4),
+                    rhs_scale=x_sc[:, s, g, toks],
                     start=(g == 0),
                     stop=(g == 1),
                 )
             return ps
 
-        def k_units(b):
-            e_tiles[b] = stage.tile([P, HB, T], F32, name="e_t", tag="e_t", bufs=K_FIRST + 1)
+        def k_units(s, i):
+            e_tiles[(s, i)] = stage.tile([P, HB, N], F32, name="e_t", tag="e_t", bufs=4)
             for hb in range(HB):
-                ps = project(MK, b, hb)
-                nc.scalar.activation(out=e_tiles[b][:, hb, :], in_=ps[:], func=ACT.Exp)
+                ps = project(MK, s, i, hb)
+                nc.scalar.activation(out=e_tiles[(s, i)][:, hb, :], in_=ps[:], func=ACT.Exp)
 
-        def v_units(b):
-            if b > 0:
-                p_tiles[b] = stage.tile([P, HB, T], F32, name="p_t", tag="six", bufs=5, align_bytes=64)
+        def v_units(s, i):
+            p_tiles[(s, i)] = stage.tile([P, HB, N], F32, name="p_t", tag="six", bufs=5, align_bytes=64)
             for hb in range(HB):
-                ps = project(MV, b, hb)
+                ps = project(MV, s, i, hb)
                 nc.vector.scalar_tensor_tensor(
-                    out=n_sum[:, hb, :] if b == 0 else p_tiles[b][:, hb, :],
+                    out=p_tiles[(s, i)][:, hb, :],
                     in0=ps[:],
                     scalar=b_cols[:, HB + hb : HB + hb + 1],
-                    in1=e_tiles[b][:, hb, :],
+                    in1=e_tiles[(s, i)][:, hb, :],
                     op0=ALU.add,
                     op1=ALU.mult,
                 )
 
-        q_order = [(b, hb) for b in range(B) for hb in range(HB)]
-        q_issued = []
+        def add_exponentials(s, i):
+            if i == 0:
+                return
+            if i == 1:
+                d_sum[s] = stage.tile([P, HB, N], F32, name="d_sum", tag="d_sum", bufs=2)
+            first = e_tiles[(s, 0)] if i == 1 else d_sum[s]
+            engine = nc.gpsimd if (s, i) in G_ADD else nc.vector
+            for hb in range(HB):
+                engine.tensor_tensor(
+                    out=d_sum[s][:, hb, :], in0=first[:, hb, :], in1=e_tiles[(s, i)][:, hb, :], op=ALU.add
+                )
+            if i == PAIRS - 1:
+                fold(d_sum[s])
 
-        def q_units(n):
-            for b, hb in q_order[len(q_issued) : len(q_issued) + n]:
-                assert 2 * b + 2 <= len(quantised)
-                q_issued.append((b, hb))
-                ps = project(MQ, b, hb)
+        def fold(t):
+            nc.vector.tensor_tensor(out=t[:, :, 0:HALF], in0=t[:, :, 0:HALF], in1=t[:, :, HALF:N], op=ALU.add)
+
+        def add_products(s, i):
+            if i == 1:
+                n_sum[s] = stage.tile([P, HB, N], F32, name="n_sum", tag="n_sum", bufs=2)
+            first = p_tiles[(s, 0)] if i == 1 else n_sum[s]
+            nc.vector.tensor_tensor(out=n_sum[s][:], in0=first[:], in1=p_tiles[(s, i)][:], op=ALU.add)
+            if i == PAIRS - 1:
+                fold(n_sum[s])
+
+        def reciprocal(s):
+            d = d_sum[s][:, :, 0:HALF]
+            nc.scalar.activation(out=d, in_=d, func=ACT.Ln)
+            nc.scalar.activation(out=d, in_=d, func=ACT.Exp, scale=-1.0)
+
+        def mean_product(s):
+            nc.vector.tensor_tensor(
+                out=n_sum[s][:, :, 0:HALF], in0=n_sum[s][:, :, 0:HALF], in1=d_sum[s][:, :, 0:HALF], op=ALU.mult
+            )
+
+        def mean_transpose(s):
+            hw[s] = stage.tile([P, 2 * JH, H], F32, name="hw", tag="hw", bufs=2)
+            for j in range(JH):
+                ps = bank()
+                for hb in range(HB):
+                    nc.tensor.transpose(ps[:, hb * P : (hb + 1) * P], n_sum[s][:, hb, j * P : (j + 1) * P], ident[:])
+                for k in range(2):
+                    nc.scalar.mul(out=hw[s][:, JH * k + j, :], in_=ps[:, 0:H], mul=0.5)
+
+        def q_units(s, i, hbs=range(HB)):
+            for hb in hbs:
+                th_tiles[(s, i, hb)] = stage.tile([P, N], F32, name="th", tag="th", bufs=12)
+                ps = project(MQ, s, i, hb)
                 nc.scalar.activation(
-                    out=th[:, b, hb, :], in_=ps[:], func=ACT.Tanh, bias=b_cols[:, hb : hb + 1], scale=0.5
+                    out=th_tiles[(s, i, hb)][:], in_=ps[:], func=ACT.Tanh, bias=b_cols[:, hb : hb + 1], scale=0.5
                 )
 
-        def add_exponentials(b):
-            if b >= 1:
-                first = e_tiles[0][:] if b == 1 else d_sum[:]
-                nc.vector.tensor_tensor(out=d_sum[:], in0=first, in1=e_tiles[b][:], op=ALU.add)
-
-        def add_products(b, hbs):
-            if b >= 1:
-                nc.vector.tensor_tensor(
-                    out=n_sum[:, hbs, :], in0=n_sum[:, hbs, :], in1=p_tiles[b][:, hbs, :], op=ALU.add
+        def finish(s, i, fine=False):
+            o_sb = stage.tile([P, 2 * JH, H], F32, name="o_sb", tag="o_sb", bufs=3)
+            for hb in range(HB):
+                ps = bank()
+                for c in range(2 * JH):
+                    nc.tensor.transpose(ps[:, c * P : (c + 1) * P], th_tiles[(s, i, hb)][:, c * P : (c + 1) * P], ident[:])
+                cols = slice(hb * P, (hb + 1) * P)
+                nc.vector.scalar_tensor_tensor(
+                    out=o_sb[:, :, cols],
+                    in0=ps[:].rearrange("p (c h) -> p c h", c=2 * JH),
+                    scalar=1.0,
+                    in1=hw[s][:, :, cols],
+                    op0=ALU.add,
+                    op1=ALU.mult,
                 )
+                if fine:
+                    for k in range(2):
+                        nc.sync.dma_start(out=out[2 * i + k].rearrange("(p j) h -> p j h", j=J)[:, JH * s : JH * (s + 1), cols], in_=o_sb[:, JH * k : JH * (k + 1), cols])
+            if not fine:
+                for k in range(2):
+                    nc.sync.dma_start(out=out[2 * i + k].rearrange("(p j) h -> p j h", j=J)[:, JH * s : JH * (s + 1), :], in_=o_sb[:, JH * k : JH * (k + 1), :])
 
-        def tokens_to_partitions(src):
+        def bias_columns():
+            nc.vector.tensor_copy(out=b_rows32[:], in_=b_rows[:])
             ps = bank()
-            for j in range(J):
-                nc.tensor.transpose(ps[:, j * P : (j + 1) * P], src[:, j * P : (j + 1) * P], ident[:])
-            return ps
-
-        def weighted_mean(hb):
-            nc.vector.tensor_tensor(out=n_sum[:, hb, :], in0=n_sum[:, hb, :], in1=d_sum[:, hb, :], op=ALU.mult)
-            q_units(Q_IN_MEAN[0])
-            ps = tokens_to_partitions(n_sum[:, hb, :])
-            q_units(Q_IN_MEAN[1])
-            nc.scalar.mul(
-                out=hw[:, :, hb * P : (hb + 1) * P], in_=ps[:].rearrange("p (j h) -> p j h", j=J), mul=0.5
-            )
-
-        def transpose_tanh(b, hb):
-            tanh_banks[(b, hb)] = tokens_to_partitions(th[:, b, hb, :])
-
-        def finish(b, hb):
-            if b not in o_tiles:
-                o_tiles[b] = stage.tile([P, J, H], F32, name="o_sb", tag="x_raw", bufs=X_BUFS)
-            cols = slice(hb * P, (hb + 1) * P)
-            nc.vector.scalar_tensor_tensor(
-                out=o_tiles[b][:, :, cols],
-                in0=tanh_banks[(b, hb)][:].rearrange("p (j h) -> p j h", j=J),
-                scalar=1.0,
-                in1=hw[:, :, cols],
-                op0=ALU.add,
-                op1=ALU.mult,
-            )
-            dst = out[b].rearrange("(p j) h -> p j h", j=J)
-            if b == B - 1:
-                nc.sync.dma_start(out=dst[:, :, cols], in_=o_tiles[b][:, :, cols])
-            elif hb == HB - 1:
-                nc.sync.dma_start(out=dst, in_=o_tiles[b][:])
+            nc.tensor.transpose(ps[:, 0:P], b_rows32[:], ident[:])
+            nc.vector.tensor_scalar_mul(out=b_cols[:, 0:HB], in0=ps[:, 0:HB], scalar1=0.5)
+            nc.vector.tensor_copy(out=b_cols[:, HB : 2 * HB], in_=ps[:, HB : 2 * HB])
 
         nc.vector.memset(b_rows[:], 0.0)
         nc.scalar.dma_start(out=b_rows[0:HB, :], in_=bq.rearrange("(r c) -> r c", c=P))
@@ -243,83 +259,99 @@ def tile_aftattention_t_kernel(tc, x, Wq, bq, Wk, bk, Wv, bv, wbias, out):
         nc.vector.memset(warm[:], 0.0)
         nc.scalar.activation(out=warm[:], in_=warm[:], func=ACT.Exp)
 
-        load_x(0, 2)
+        load_x(0, 0, 1)
         load_w(MK)
+        load_x(0, 1, 1)
         load_w(MV)
-        load_x(1, 2)
-        load_x(2, 2)
-        load_x(3, 1)
-
-        transpose_x_upto(2)
+        load_x(0, 2, 1)
         load_w(MQ)
-        quantise_x_upto(1)
-        transpose_w(MK, 0, "v")
-        quantise_w(MK, 0)
-        quantise_x_upto(2)
+        load_x(0, 3, 1)
+        transpose_x(0, 0, "svsv")
+        quantise_x(0, 0, 2)
+        transpose_w(MK, 0, "s")
         transpose_w(MK, 1, "v")
+        quantise_w(MK, 0)
         transpose_w(MK, 2, "s")
         quantise_w(MK, 1)
         quantise_w(MK, 2)
+        transpose_x(0, 1)
+        load_x(1, 0, 1)
+        k_units(0, 0)
+        quantise_x(0, 1)
         transpose_w(MV, 0, "s")
-        nc.vector.tensor_copy(out=b_rows32[:], in_=b_rows[:])
-        quantise_w(MV, 0)
-        k_units(0)
         transpose_w(MV, 1, "v")
         transpose_w(MV, 2, "s")
-        ps_b = bank()
-        nc.tensor.transpose(ps_b[:, 0:P], b_rows32[:], ident[:])
-        transpose_x_upto(4)
+        bias_columns()
+        quantise_w(MV, 0)
         quantise_w(MV, 1)
         quantise_w(MV, 2)
-        nc.vector.tensor_scalar_mul(out=b_cols[:, 0:HB], in0=ps_b[:, 0:HB], scalar1=0.5)
-        nc.vector.tensor_copy(out=b_cols[:, HB : 2 * HB], in_=ps_b[:, HB : 2 * HB])
-        quantise_x_upto(4)
-        v_units(0)
-        q_units(Q_AFTER_EARLY[0])
-
-        for b in range(1, EARLY):
-            transpose_x_upto(3 * b + 2)
-            k_units(b)
-            if b == 2:
-                for r in range(HB):
-                    transpose_w(MQ, r, "s")
-            add_products(b - 1, slice(0, HB))
-            quantise_x_upto(3 * b + 2)
-            transpose_x_upto(3 * b + 4)
-            add_exponentials(b)
-            v_units(b)
-            quantise_x_upto(3 * b + 3)
-            if b == 2:
-                for r in range(HB):
-                    quantise_w(MQ, r)
-            q_units(Q_AFTER_EARLY[b])
-        add_products(EARLY - 1, slice(0, HB))
-        quantise_x_upto(PAIRS)
-
-        for b in range(EARLY, B):
-            k_units(b)
-            add_exponentials(b)
-            q_units(Q_AFTER_LATE_K[b - EARLY])
-        for hb in range(HB):
-            nc.scalar.activation(out=d_sum[:, hb, :], in_=d_sum[:, hb, :], func=ACT.Ln)
-        for hb in range(HB):
-            nc.scalar.activation(out=d_sum[:, hb, :], in_=d_sum[:, hb, :], func=ACT.Exp, scale=-1.0)
-        for b in range(EARLY, B):
-            v_units(b)
-        q_units(Q_AFTER_LATE_V)
-
-        last = [(2 * bb + b, hb) for bb in range(B // 2) for hb in range(HB) for b in range(2)]
-        for b, hb in last[:TANH_BEFORE_MEAN]:
-            transpose_tanh(b, hb)
-        for hb in range(HB):
-            for b in range(EARLY, B):
-                add_products(b, slice(hb, hb + 1))
-            weighted_mean(hb)
-        for b, hb in last[TANH_BEFORE_MEAN:TANH_AHEAD]:
-            transpose_tanh(b, hb)
-        for n in range(len(last)):
-            finish(last[n][0], last[n][1])
-            if n == 0:
-                q_units(len(q_order))
-            if n + TANH_AHEAD < len(last):
-                transpose_tanh(last[n + TANH_AHEAD][0], last[n + TANH_AHEAD][1])
+        transpose_x(0, 2)
+        load_x(1, 1, 1)
+        k_units(0, 1)
+        quantise_x(0, 2)
+        v_units(0, 0)
+        add_exponentials(0, 1)
+        transpose_w(MQ, 0, "s")
+        transpose_w(MQ, 1, "s")
+        transpose_w(MQ, 2, "s")
+        transpose_x(0, 3)
+        load_x(1, 2, 1)
+        k_units(0, 2)
+        quantise_w(MQ, 0)
+        quantise_w(MQ, 1)
+        quantise_w(MQ, 2)
+        quantise_x(0, 3)
+        v_units(0, 1)
+        add_exponentials(0, 2)
+        k_units(0, 3)
+        add_products(0, 1)
+        q_units(0, 0)
+        add_exponentials(0, 3)
+        v_units(0, 2)
+        transpose_x(1, 0)
+        load_x(1, 3, 1)
+        reciprocal(0)
+        quantise_x(1, 0)
+        v_units(0, 3)
+        add_products(0, 2)
+        transpose_x(1, 1)
+        add_products(0, 3)
+        mean_product(0)
+        k_units(1, 0)
+        quantise_x(1, 1)
+        q_units(0, 1)
+        v_units(1, 0)
+        mean_transpose(0)
+        finish(0, 0)
+        transpose_x(1, 2)
+        k_units(1, 1)
+        q_units(0, 2)
+        quantise_x(1, 2)
+        finish(0, 1)
+        add_exponentials(1, 1)
+        v_units(1, 1)
+        transpose_x(1, 3)
+        k_units(1, 2)
+        quantise_x(1, 3)
+        add_exponentials(1, 2)
+        add_products(1, 1)
+        q_units(0, 3)
+        v_units(1, 2)
+        finish(0, 2)
+        k_units(1, 3)
+        add_exponentials(1, 3)
+        add_products(1, 2)
+        v_units(1, 3)
+        reciprocal(1)
+        add_products(1, 3)
+        mean_product(1)
+        q_units(1, 0)
+        finish(0, 3)
+        q_units(1, 1)
+        q_units(1, 2)
+        mean_transpose(1)
+        finish(1, 0)
+        q_units(1, 3)
+        finish(1, 1)
+        finish(1, 2)
+        finish(1, 3, True)

@@ -259,99 +259,99 @@ def tile_aftattention_t_kernel(tc, x, Wq, bq, Wk, bk, Wv, bv, wbias, out):
         nc.vector.memset(warm[:], 0.0)
         nc.scalar.activation(out=warm[:], in_=warm[:], func=ACT.Exp)
 
-        load_x(0, 0, 1)
         load_w(MK)
+        load_x(0, 0, 1)
         load_x(0, 1, 1)
         load_w(MV)
         load_x(0, 2, 1)
-        load_w(MQ)
         load_x(0, 3, 1)
-        transpose_x(0, 0, "svsv")
-        quantise_x(0, 0, 2)
+        load_w(MQ)
         transpose_w(MK, 0, "s")
         transpose_w(MK, 1, "v")
-        quantise_w(MK, 0)
         transpose_w(MK, 2, "s")
+        transpose_x(0, 0, "svsv")
+        load_x(1, 0, 1)
+        quantise_x(0, 0, 2)
+        quantise_w(MK, 0)
         quantise_w(MK, 1)
         quantise_w(MK, 2)
         transpose_x(0, 1)
-        load_x(1, 0, 1)
-        k_units(0, 0)
-        quantise_x(0, 1)
+        load_x(1, 1, 1)
         transpose_w(MV, 0, "s")
         transpose_w(MV, 1, "v")
         transpose_w(MV, 2, "s")
+        transpose_x(0, 2, "vsss")
+        load_x(1, 2, 1)
+        quantise_x(0, 1)
+        transpose_x(0, 3)
+        load_x(1, 3, 1)
+        quantise_x(0, 2)
         bias_columns()
+        k_units(0, 0)
+        k_units(0, 1)
+        quantise_x(0, 3)
+        add_exponentials(0, 1)
+        k_units(0, 2)
+        k_units(0, 3)
         quantise_w(MV, 0)
         quantise_w(MV, 1)
         quantise_w(MV, 2)
-        transpose_x(0, 2)
-        load_x(1, 1, 1)
-        k_units(0, 1)
-        quantise_x(0, 2)
-        v_units(0, 0)
-        add_exponentials(0, 1)
+        add_exponentials(0, 2)
+        add_exponentials(0, 3)
         transpose_w(MQ, 0, "s")
         transpose_w(MQ, 1, "s")
         transpose_w(MQ, 2, "s")
-        transpose_x(0, 3)
-        load_x(1, 2, 1)
-        k_units(0, 2)
+        transpose_x(1, 0)
+        v_units(0, 0)
+        v_units(0, 1)
         quantise_w(MQ, 0)
         quantise_w(MQ, 1)
         quantise_w(MQ, 2)
-        quantise_x(0, 3)
-        v_units(0, 1)
-        add_exponentials(0, 2)
-        k_units(0, 3)
         add_products(0, 1)
-        q_units(0, 0)
-        add_exponentials(0, 3)
-        v_units(0, 2)
-        transpose_x(1, 0)
-        load_x(1, 3, 1)
         reciprocal(0)
-        quantise_x(1, 0)
+        v_units(0, 2)
         v_units(0, 3)
-        add_products(0, 2)
+        q_units(0, 0)
+        quantise_x(1, 0)
         transpose_x(1, 1)
-        add_products(0, 3)
-        mean_product(0)
-        k_units(1, 0)
+        add_products(0, 2)
         quantise_x(1, 1)
-        q_units(0, 1)
+        transpose_x(1, 2)
+        k_units(1, 0)
+        add_products(0, 3)
+        k_units(1, 1)
+        quantise_x(1, 2)
+        add_exponentials(1, 1)
+        mean_product(0)
         v_units(1, 0)
+        v_units(1, 1)
         mean_transpose(0)
         finish(0, 0)
-        transpose_x(1, 2)
-        k_units(1, 1)
-        q_units(0, 2)
-        quantise_x(1, 2)
-        finish(0, 1)
-        add_exponentials(1, 1)
-        v_units(1, 1)
         transpose_x(1, 3)
-        k_units(1, 2)
         quantise_x(1, 3)
-        add_exponentials(1, 2)
+        q_units(0, 1)
         add_products(1, 1)
-        q_units(0, 3)
-        v_units(1, 2)
-        finish(0, 2)
+        k_units(1, 2)
         k_units(1, 3)
+        add_exponentials(1, 2)
         add_exponentials(1, 3)
+        v_units(1, 2)
         add_products(1, 2)
+        q_units(0, 2)
+        finish(0, 1)
+        q_units(0, 3)
         v_units(1, 3)
+        finish(0, 2)
         reciprocal(1)
+        q_units(1, 0)
         add_products(1, 3)
         mean_product(1)
-        q_units(1, 0)
         finish(0, 3)
         q_units(1, 1)
         q_units(1, 2)
         mean_transpose(1)
         finish(1, 0)
-        q_units(1, 3)
         finish(1, 1)
+        q_units(1, 3)
         finish(1, 2)
         finish(1, 3, True)

@@ -24,6 +24,7 @@ FLOPS = 2 * B * T * DM * 3 * H
 MK, MV, MQ = 0, 1, 2
 PERM = ()
 S_PERM = ()
+G_STEP = 256
 G_ADD = ()
 
 
@@ -179,10 +180,13 @@ def tile_aftattention_t_kernel(tc, x, Wq, bq, Wk, bk, Wv, bv, wbias, out):
                 d_sum[s] = stage.tile([P, HB, N], F32, name="d_sum", tag="d_sum", bufs=2)
             first = e_tiles[(s, 0)] if i == 1 else d_sum[s]
             engine = nc.gpsimd if (s, i) in G_ADD else nc.vector
+            step = G_STEP if (s, i) in G_ADD else N
             for hb in range(HB):
-                engine.tensor_tensor(
-                    out=d_sum[s][:, hb, :], in0=first[:, hb, :], in1=e_tiles[(s, i)][:, hb, :], op=ALU.add
-                )
+                for c in range(0, N, step):
+                    cols = slice(c, c + step)
+                    engine.tensor_tensor(
+                        out=d_sum[s][:, hb, cols], in0=first[:, hb, cols], in1=e_tiles[(s, i)][:, hb, cols], op=ALU.add
+                    )
             if i == PAIRS - 1:
                 fold(d_sum[s])
 
@@ -277,81 +281,81 @@ def tile_aftattention_t_kernel(tc, x, Wq, bq, Wk, bk, Wv, bv, wbias, out):
         quantise_w(MK, 2)
         transpose_x(0, 1)
         load_x(1, 1, 1)
+        quantise_x(0, 1)
         transpose_w(MV, 0, "s")
         transpose_w(MV, 1, "v")
         transpose_w(MV, 2, "s")
         transpose_x(0, 2, "vsss")
         load_x(1, 2, 1)
-        quantise_x(0, 1)
+        quantise_w(MV, 0)
+        quantise_w(MV, 1)
+        quantise_w(MV, 2)
         transpose_x(0, 3)
         load_x(1, 3, 1)
-        quantise_x(0, 2)
         bias_columns()
+        quantise_x(0, 2)
         k_units(0, 0)
         k_units(0, 1)
         quantise_x(0, 3)
         add_exponentials(0, 1)
         k_units(0, 2)
         k_units(0, 3)
-        quantise_w(MV, 0)
-        quantise_w(MV, 1)
-        quantise_w(MV, 2)
         add_exponentials(0, 2)
         add_exponentials(0, 3)
         transpose_w(MQ, 0, "s")
         transpose_w(MQ, 1, "s")
         transpose_w(MQ, 2, "s")
-        transpose_x(1, 0)
-        v_units(0, 0)
-        v_units(0, 1)
         quantise_w(MQ, 0)
         quantise_w(MQ, 1)
         quantise_w(MQ, 2)
-        add_products(0, 1)
+        transpose_x(1, 0)
         reciprocal(0)
+        v_units(0, 0)
+        v_units(0, 1)
         v_units(0, 2)
-        v_units(0, 3)
-        q_units(0, 0)
+        add_products(0, 1)
         quantise_x(1, 0)
-        transpose_x(1, 1)
         add_products(0, 2)
+        transpose_x(1, 1)
+        v_units(0, 3)
         quantise_x(1, 1)
         transpose_x(1, 2)
-        k_units(1, 0)
         add_products(0, 3)
-        k_units(1, 1)
         quantise_x(1, 2)
-        add_exponentials(1, 1)
+        q_units(0, 0)
         mean_product(0)
+        k_units(1, 0)
+        k_units(1, 1)
         v_units(1, 0)
         v_units(1, 1)
-        mean_transpose(0)
-        finish(0, 0)
         transpose_x(1, 3)
-        quantise_x(1, 3)
-        q_units(0, 1)
+        add_exponentials(1, 1)
+        mean_transpose(0)
         add_products(1, 1)
+        quantise_x(1, 3)
         k_units(1, 2)
-        k_units(1, 3)
-        add_exponentials(1, 2)
-        add_exponentials(1, 3)
         v_units(1, 2)
+        add_exponentials(1, 2)
+        finish(0, 0)
+        q_units(0, 1)
         add_products(1, 2)
+        k_units(1, 3)
         q_units(0, 2)
-        finish(0, 1)
         q_units(0, 3)
+        add_exponentials(1, 3)
         v_units(1, 3)
-        finish(0, 2)
         reciprocal(1)
-        q_units(1, 0)
+        finish(0, 1)
         add_products(1, 3)
+        finish(0, 2)
+        q_units(1, 0)
+        q_units(1, 1)
         mean_product(1)
         finish(0, 3)
-        q_units(1, 1)
-        q_units(1, 2)
         mean_transpose(1)
         finish(1, 0)
         finish(1, 1)
-        q_units(1, 3)
+        q_units(1, 2)
         finish(1, 2)
+        q_units(1, 3)
         finish(1, 3, True)

@@ -14,17 +14,14 @@ ALU = mybir.AluOpType
 B, T, DM, H = 8, 512, 1024, 384
 P = 128
 J = T // P
-JH = J // 2
 HB = H // P
-PAIRS = B // 2
-N = 512
-HALF = N // 2
+BU = 4
+N = BU * P
+UNITS = B * J // BU
 FLOPS = 2 * B * T * DM * 3 * H
 
 MK, MV, MQ = 0, 1, 2
-PERM = ()
 S_PERM = ()
-G_STEP = 256
 G_ADD = ()
 
 
@@ -44,12 +41,13 @@ def tile_aftattention_t_kernel(tc, x, Wq, bq, Wk, bk, Wv, bv, wbias, out):
 
         w_codes = keep.tile([P, 3, 2 * H], U32, name="w_codes", align_bytes=64)
         w_sc = keep.tile([P, 3, 2 * H], U8, name="w_sc", align_bytes=64)
-        x_codes = keep.tile([P, 2, 2, B * HALF], U32, name="x_codes", align_bytes=64)
-        x_sc = keep.tile([P, 2, 2, B * HALF], U8, name="x_sc", align_bytes=64)
+        x_codes = keep.tile([P, UNITS, 2, N], U32, name="x_codes", align_bytes=64)
+        x_sc = keep.tile([P, UNITS, 2, N], U8, name="x_sc", align_bytes=64)
         b_rows = keep.tile([P, P], BF16, name="b_rows")
         b_rows32 = keep.tile([P, P], F32, name="b_rows32")
         b_cols = keep.tile([P, 8], F32, name="b_cols")
         warm = keep.tile([P, 1], F32, name="warm")
+        d_sum = keep.tile([P, J, HB, P], F32, name="d_sum")
 
         w_dram = (Wk, Wv, Wq)
         w_raw = {}
@@ -59,34 +57,33 @@ def tile_aftattention_t_kernel(tc, x, Wq, bq, Wk, bk, Wv, bv, wbias, out):
         x_grp = {}
         e_tiles = {}
         p_tiles = {}
-        d_sum = {}
         n_sum = {}
         hw = {}
         th_tiles = {}
-        tanh_banks = {}
 
         def load_w(m):
             w_raw[m] = stage.tile([P, HB, DM], BF16, name="w_raw", tag="six", bufs=5, align_bytes=64)
             for r in range(HB):
                 nc.sync.dma_start(out=w_raw[m][:, r, :], in_=w_dram[m][r * P : (r + 1) * P, :])
 
-        def load_x(s, i, parts):
-            x_raw[(s, i)] = stage.tile([P, 2, JH, DM], BF16, name="x_raw", tag="x_raw", bufs=4)
-            for k in range(2):
-                src = x[2 * i + k].rearrange("(p j) k -> p j k", j=J)[:, JH * s : JH * (s + 1), :]
-                for c in range(parts):
-                    js = slice(c * JH // parts, (c + 1) * JH // parts)
-                    nc.sync.dma_start(out=x_raw[(s, i)][:, k, js, :], in_=src[:, js, :])
+        def batches(u):
+            return slice(BU * (u % 2), BU * (u % 2) + BU)
 
-        def permute_x(s, i):
+        def load_x(u):
+            x_raw[u] = stage.tile([P, BU, DM], BF16, name="x_raw", tag="x_raw", bufs=4)
+            src = x[batches(u)].rearrange("b (p j) k -> p j b k", j=J)[:, u // 2]
+            for k in range(0, BU, 2):
+                nc.sync.dma_start(out=x_raw[u][:, k : k + 2, :], in_=src[:, k : k + 2, :])
+
+        def permute_x(u):
             for k in range(2):
-                x_perm[(s, i, k)] = stage.tile([P, JH * DM // 2], F32, name="x_perm", tag="x_perm", bufs=3)
-                (nc.scalar.copy if (s, i) in S_PERM else nc.vector.tensor_copy)(
-                    out=x_perm[(s, i, k)][:].rearrange("p (jg u w) -> p jg u w", jg=2 * JH, u=2),
-                    in_=x_raw[(s, i)][:, k, :, :]
+                x_perm[(u, k)] = stage.tile([P, 2 * DM // 2], F32, name="x_perm", tag="x_perm", bufs=3)
+                (nc.scalar.copy if u in S_PERM else nc.vector.tensor_copy)(
+                    out=x_perm[(u, k)][:].rearrange("p (jg u w) -> p jg u w", jg=4, u=2),
+                    in_=x_raw[u][:, 2 * k : 2 * k + 2, :]
                     .rearrange("p j k -> p (j k)")
                     .bitcast(F32)
-                    .rearrange("p (jg w u) -> p jg u w", jg=2 * JH, u=2),
+                    .rearrange("p (jg w u) -> p jg u w", jg=4, u=2),
                 )
 
         def transpose_words(dst_bank, words, permuted):
@@ -116,142 +113,128 @@ def tile_aftattention_t_kernel(tc, x, Wq, bq, Wk, bk, Wv, bv, wbias, out):
                     in_=w_grp[m][:, 4 * (g * H + r * P) : 4 * (g * H + (r + 1) * P)],
                 )
 
-        def transpose_x(s, i, engines="ssss"):
-            x_grp[(s, i)] = stage.tile([P, 2 * N * 4], BF16, name="x_grp", tag="x_grp", bufs=2, align_bytes=64)
-            grp32 = x_grp[(s, i)][:].bitcast(F32).rearrange("p (g c u) -> p g c u", g=2, u=2)
-            for c in range(2 * JH):
+        def transpose_x(u, engines="ssss"):
+            x_grp[u] = stage.tile([P, 2 * N * 4], BF16, name="x_grp", tag="x_grp", bufs=2, align_bytes=64)
+            grp32 = x_grp[u][:].bitcast(F32).rearrange("p (g c u) -> p g c u", g=2, u=2)
+            for c in range(BU):
                 ps = bank()
-                if (s, i, 0) in x_perm:
-                    transpose_words(ps, x_perm[(s, i, c // JH)][:, (c % JH) * 512 : (c % JH + 1) * 512], True)
+                if (u, 0) in x_perm:
+                    transpose_words(ps, x_perm[(u, c // 2)][:, (c % 2) * 512 : (c % 2 + 1) * 512], True)
                 else:
-                    transpose_words(ps, x_raw[(s, i)][:, c // JH, c % JH, :].bitcast(F32), False)
+                    transpose_words(ps, x_raw[u][:, c, :].bitcast(F32), False)
                 copy_grouped(engines[c], grp32[:, :, c * P : (c + 1) * P, :], ps)
 
-        def quantise_x(s, i, parts=1):
+        def quantise_x(u, parts=1):
             for c in range(parts):
                 w = N // parts
                 for g in range(2):
-                    cols = slice(i * N + c * w, i * N + (c + 1) * w)
                     nc.vector.quantize_mx(
-                        out=x_codes[:, s, g, cols].bitcast(FP8X4),
-                        scales=x_sc[:, s, g, cols],
-                        in_=x_grp[(s, i)][:, 4 * (g * N + c * w) : 4 * (g * N + (c + 1) * w)],
+                        out=x_codes[:, u, g, c * w : (c + 1) * w].bitcast(FP8X4),
+                        scales=x_sc[:, u, g, c * w : (c + 1) * w],
+                        in_=x_grp[u][:, 4 * (g * N + c * w) : 4 * (g * N + (c + 1) * w)],
                     )
 
-        def project(m, s, i, hb):
+        def project(m, u, hb):
             ps = bank()
             for g in range(2):
                 cols = slice(g * H + hb * P, g * H + (hb + 1) * P)
-                toks = slice(i * N, (i + 1) * N)
                 nc.tensor.matmul_mx(
                     out=ps[:],
                     lhsT=w_codes[:, m, cols].bitcast(FP8X4),
                     lhsT_scale=w_sc[:, m, cols],
-                    rhs=x_codes[:, s, g, toks].bitcast(FP8X4),
-                    rhs_scale=x_sc[:, s, g, toks],
+                    rhs=x_codes[:, u, g, :].bitcast(FP8X4),
+                    rhs_scale=x_sc[:, u, g, :],
                     start=(g == 0),
                     stop=(g == 1),
                 )
             return ps
 
-        def k_units(s, i):
-            e_tiles[(s, i)] = stage.tile([P, HB, N], F32, name="e_t", tag="e_t", bufs=4)
+        def k_units(u):
+            e_tiles[u] = stage.tile([P, HB, N], F32, name="e_t", tag="e_t", bufs=4)
             for hb in range(HB):
-                ps = project(MK, s, i, hb)
-                nc.scalar.activation(out=e_tiles[(s, i)][:, hb, :], in_=ps[:], func=ACT.Exp)
+                ps = project(MK, u, hb)
+                nc.scalar.activation(out=e_tiles[u][:, hb, :], in_=ps[:], func=ACT.Exp)
 
-        def v_units(s, i):
-            p_tiles[(s, i)] = stage.tile([P, HB, N], F32, name="p_t", tag="six", bufs=5, align_bytes=64)
+        def v_units(u):
+            p_tiles[u] = stage.tile([P, HB, N], F32, name="p_t", tag="six", bufs=5, align_bytes=64)
             for hb in range(HB):
-                ps = project(MV, s, i, hb)
+                ps = project(MV, u, hb)
                 nc.vector.scalar_tensor_tensor(
-                    out=p_tiles[(s, i)][:, hb, :],
+                    out=p_tiles[u][:, hb, :],
                     in0=ps[:],
                     scalar=b_cols[:, HB + hb : HB + hb + 1],
-                    in1=e_tiles[(s, i)][:, hb, :],
+                    in1=e_tiles[u][:, hb, :],
                     op0=ALU.add,
                     op1=ALU.mult,
                 )
 
-        def add_exponentials(s, i):
-            if i == 0:
-                return
-            if i == 1:
-                d_sum[s] = stage.tile([P, HB, N], F32, name="d_sum", tag="d_sum", bufs=2)
-            first = e_tiles[(s, 0)] if i == 1 else d_sum[s]
-            engine = nc.gpsimd if (s, i) in G_ADD else nc.vector
-            step = G_STEP if (s, i) in G_ADD else N
+        def batch_sum(engine, dst, a, b, t):
             for hb in range(HB):
-                for c in range(0, N, step):
-                    cols = slice(c, c + step)
-                    engine.tensor_tensor(
-                        out=d_sum[s][:, hb, cols], in0=first[:, hb, cols], in1=e_tiles[(s, i)][:, hb, cols], op=ALU.add
-                    )
-            if i == PAIRS - 1:
-                fold(d_sum[s])
+                engine.tensor_tensor(out=t[:, hb, :], in0=a[:, hb, :], in1=b[:, hb, :], op=ALU.add)
+            for hb in range(HB):
+                engine.tensor_tensor(
+                    out=t[:, hb, 0 : N // 2], in0=t[:, hb, 0 : N // 2], in1=t[:, hb, N // 2 : N], op=ALU.add
+                )
+            for hb in range(HB):
+                engine.tensor_tensor(out=dst[:, hb, :], in0=t[:, hb, 0:P], in1=t[:, hb, P : 2 * P], op=ALU.add)
 
-        def fold(t):
-            nc.vector.tensor_tensor(out=t[:, :, 0:HALF], in0=t[:, :, 0:HALF], in1=t[:, :, HALF:N], op=ALU.add)
+        def sum_exponentials(j):
+            t = stage.tile([P, HB, N], F32, name="sum_t", tag="sum_t", bufs=2)
+            batch_sum(nc.gpsimd if j in G_ADD else nc.vector, d_sum[:, j, :, :], e_tiles[2 * j], e_tiles[2 * j + 1], t)
 
-        def add_products(s, i):
-            if i == 1:
-                n_sum[s] = stage.tile([P, HB, N], F32, name="n_sum", tag="n_sum", bufs=2)
-            first = p_tiles[(s, 0)] if i == 1 else n_sum[s]
-            nc.vector.tensor_tensor(out=n_sum[s][:], in0=first[:], in1=p_tiles[(s, i)][:], op=ALU.add)
-            if i == PAIRS - 1:
-                fold(n_sum[s])
+        def sum_products(j):
+            t = stage.tile([P, HB, N], F32, name="sum_t", tag="sum_t", bufs=2)
+            n_sum[j] = stage.tile([P, HB, P], F32, name="n_sum", tag="n_sum", bufs=3)
+            batch_sum(nc.vector, n_sum[j][:], p_tiles[2 * j], p_tiles[2 * j + 1], t)
 
-        def reciprocal(s):
-            d = d_sum[s][:, :, 0:HALF]
+        def reciprocal(j0, j1):
+            d = d_sum[:, j0:j1, :, :]
             nc.scalar.activation(out=d, in_=d, func=ACT.Ln)
             nc.scalar.activation(out=d, in_=d, func=ACT.Exp, scale=-1.0)
 
-        def mean_product(s):
-            nc.vector.tensor_tensor(
-                out=n_sum[s][:, :, 0:HALF], in0=n_sum[s][:, :, 0:HALF], in1=d_sum[s][:, :, 0:HALF], op=ALU.mult
-            )
+        def mean_product(j):
+            nc.vector.tensor_tensor(out=n_sum[j][:], in0=n_sum[j][:], in1=d_sum[:, j, :, :], op=ALU.mult)
 
-        def mean_transpose(s):
-            hw[s] = stage.tile([P, 2 * JH, H], F32, name="hw", tag="hw", bufs=2)
-            for j in range(JH):
-                ps = bank()
-                for hb in range(HB):
-                    nc.tensor.transpose(ps[:, hb * P : (hb + 1) * P], n_sum[s][:, hb, j * P : (j + 1) * P], ident[:])
-                for k in range(2):
-                    nc.scalar.mul(out=hw[s][:, JH * k + j, :], in_=ps[:, 0:H], mul=0.5)
+        def mean_transpose(j):
+            hw[j] = stage.tile([P, H], F32, name="hw", tag="hw", bufs=3)
+            ps = bank()
+            for hb in range(HB):
+                nc.tensor.transpose(ps[:, hb * P : (hb + 1) * P], n_sum[j][:, hb, :], ident[:])
+            nc.scalar.mul(out=hw[j][:], in_=ps[:, 0:H], mul=0.5)
 
-        def q_units(s, i, hbs=range(HB)):
-            for hb in hbs:
-                th_tiles[(s, i, hb)] = stage.tile([P, N], F32, name="th", tag="th", bufs=12)
-                ps = project(MQ, s, i, hb)
+        def q_units(u):
+            for hb in range(HB):
+                th_tiles[(u, hb)] = stage.tile([P, N], F32, name="th", tag="th", bufs=12)
+                ps = project(MQ, u, hb)
                 nc.scalar.activation(
-                    out=th_tiles[(s, i, hb)][:], in_=ps[:], func=ACT.Tanh, bias=b_cols[:, hb : hb + 1], scale=0.5
+                    out=th_tiles[(u, hb)][:], in_=ps[:], func=ACT.Tanh, bias=b_cols[:, hb : hb + 1], scale=0.5
                 )
 
-        def finish(s, i, fine=False):
-            o_sb = stage.tile([P, 2 * JH, H], F32, name="o_sb", tag="o_sb", bufs=3)
+        def finish(u, fine=False):
+            o_sb = stage.tile([P, BU, H], F32, name="o_sb", tag="o_sb", bufs=3)
+            dst = out[batches(u)].rearrange("b (p j) h -> p j b h", j=J)[:, u // 2]
             for hb in range(HB):
                 ps = bank()
-                for c in range(2 * JH):
-                    nc.tensor.transpose(ps[:, c * P : (c + 1) * P], th_tiles[(s, i, hb)][:, c * P : (c + 1) * P], ident[:])
+                for c in range(BU):
+                    nc.tensor.transpose(ps[:, c * P : (c + 1) * P], th_tiles[(u, hb)][:, c * P : (c + 1) * P], ident[:])
                 cols = slice(hb * P, (hb + 1) * P)
                 nc.vector.scalar_tensor_tensor(
                     out=o_sb[:, :, cols],
-                    in0=ps[:].rearrange("p (c h) -> p c h", c=2 * JH),
+                    in0=ps[:].rearrange("p (c h) -> p c h", c=BU),
                     scalar=1.0,
-                    in1=hw[s][:, :, cols],
+                    in1=hw[u // 2][:, cols].unsqueeze(1).to_broadcast([P, BU, P]),
                     op0=ALU.add,
                     op1=ALU.mult,
                 )
                 if fine:
-                    for k in range(2):
-                        nc.sync.dma_start(out=out[2 * i + k].rearrange("(p j) h -> p j h", j=J)[:, JH * s : JH * (s + 1), cols], in_=o_sb[:, JH * k : JH * (k + 1), cols])
+                    nc.sync.dma_start(out=dst[:, :, cols], in_=o_sb[:, :, cols])
             if not fine:
-                for k in range(2):
-                    nc.sync.dma_start(out=out[2 * i + k].rearrange("(p j) h -> p j h", j=J)[:, JH * s : JH * (s + 1), :], in_=o_sb[:, JH * k : JH * (k + 1), :])
+                nc.sync.dma_start(out=dst, in_=o_sb[:])
+
+        def bias_rows():
+            nc.vector.tensor_copy(out=b_rows32[:], in_=b_rows[:])
 
         def bias_columns():
-            nc.vector.tensor_copy(out=b_rows32[:], in_=b_rows[:])
             ps = bank()
             nc.tensor.transpose(ps[:, 0:P], b_rows32[:], ident[:])
             nc.vector.tensor_scalar_mul(out=b_cols[:, 0:HB], in0=ps[:, 0:HB], scalar1=0.5)
@@ -263,99 +246,101 @@ def tile_aftattention_t_kernel(tc, x, Wq, bq, Wk, bk, Wv, bv, wbias, out):
         nc.vector.memset(warm[:], 0.0)
         nc.scalar.activation(out=warm[:], in_=warm[:], func=ACT.Exp)
 
+        load_x(0)
         load_w(MK)
-        load_x(0, 0, 1)
-        load_x(0, 1, 1)
+        load_x(1)
+        load_x(2)
+        load_x(3)
         load_w(MV)
-        load_x(0, 2, 1)
-        load_x(0, 3, 1)
-        load_w(MQ)
+        transpose_x(0, "svvs")
+        load_x(4)
         transpose_w(MK, 0, "s")
+        quantise_x(0, 2)
         transpose_w(MK, 1, "v")
         transpose_w(MK, 2, "s")
-        transpose_x(0, 0, "svsv")
-        load_x(1, 0, 1)
-        quantise_x(0, 0, 2)
         quantise_w(MK, 0)
         quantise_w(MK, 1)
+        transpose_x(1, "sssv")
+        load_x(5)
         quantise_w(MK, 2)
-        transpose_x(0, 1)
-        load_x(1, 1, 1)
-        quantise_x(0, 1)
+        bias_rows()
+        quantise_x(1)
+        transpose_x(2, "svsv")
+        load_x(6)
+        transpose_x(3, "svsv")
+        load_x(7)
+        quantise_x(2)
+        bias_columns()
         transpose_w(MV, 0, "s")
         transpose_w(MV, 1, "v")
         transpose_w(MV, 2, "s")
-        transpose_x(0, 2, "vsss")
-        load_x(1, 2, 1)
+        quantise_x(3)
+        k_units(0)
+        k_units(1)
         quantise_w(MV, 0)
         quantise_w(MV, 1)
         quantise_w(MV, 2)
-        transpose_x(0, 3)
-        load_x(1, 3, 1)
-        bias_columns()
-        quantise_x(0, 2)
-        k_units(0, 0)
-        k_units(0, 1)
-        quantise_x(0, 3)
-        add_exponentials(0, 1)
-        k_units(0, 2)
-        k_units(0, 3)
-        add_exponentials(0, 2)
-        add_exponentials(0, 3)
+        sum_exponentials(0)
+        k_units(2)
+        k_units(3)
+        sum_exponentials(1)
+        reciprocal(0, 2)
+        v_units(0)
+        v_units(1)
+        v_units(2)
+        v_units(3)
+        load_w(MQ)
+        transpose_x(4)
+        sum_products(0)
+        transpose_x(5)
+        quantise_x(4)
         transpose_w(MQ, 0, "s")
         transpose_w(MQ, 1, "s")
         transpose_w(MQ, 2, "s")
+        quantise_x(5)
+        sum_products(1)
         quantise_w(MQ, 0)
+        mean_product(0)
+        mean_product(1)
+        transpose_x(6)
+        k_units(4)
+        k_units(5)
         quantise_w(MQ, 1)
         quantise_w(MQ, 2)
-        transpose_x(1, 0)
-        reciprocal(0)
-        v_units(0, 0)
-        v_units(0, 1)
-        v_units(0, 2)
-        add_products(0, 1)
-        quantise_x(1, 0)
-        add_products(0, 2)
-        transpose_x(1, 1)
-        v_units(0, 3)
-        quantise_x(1, 1)
-        transpose_x(1, 2)
-        add_products(0, 3)
-        quantise_x(1, 2)
-        q_units(0, 0)
-        mean_product(0)
-        k_units(1, 0)
-        k_units(1, 1)
-        v_units(1, 0)
-        v_units(1, 1)
-        transpose_x(1, 3)
-        add_exponentials(1, 1)
+        v_units(4)
+        q_units(0)
         mean_transpose(0)
-        add_products(1, 1)
-        quantise_x(1, 3)
-        k_units(1, 2)
-        v_units(1, 2)
-        add_exponentials(1, 2)
-        finish(0, 0)
-        q_units(0, 1)
-        add_products(1, 2)
-        k_units(1, 3)
-        q_units(0, 2)
-        q_units(0, 3)
-        add_exponentials(1, 3)
-        v_units(1, 3)
-        reciprocal(1)
-        finish(0, 1)
-        add_products(1, 3)
-        finish(0, 2)
-        q_units(1, 0)
-        q_units(1, 1)
-        mean_product(1)
-        finish(0, 3)
         mean_transpose(1)
-        finish(1, 0)
-        finish(1, 1)
-        q_units(1, 2)
-        finish(1, 2)
-        q_units(1, 3)
-        finish(1, 3, True)
+        transpose_x(7)
+        quantise_x(6)
+        sum_exponentials(2)
+        finish(0)
+        v_units(5)
+        reciprocal(2, 3)
+        k_units(6)
+        q_units(1)
+        quantise_x(7)
+        k_units(7)
+        sum_products(2)
+        v_units(6)
+        mean_product(2)
+        q_units(2)
+        q_units(3)
+        mean_transpose(2)
+        sum_exponentials(3)
+        finish(1)
+        finish(2)
+        finish(3)
+        reciprocal(3, 4)
+        v_units(7)
+        q_units(4)
+        sum_products(3)
+        q_units(5)
+        finish(4)
+        q_units(6)
+        mean_product(3)
+        finish(5)
+        mean_transpose(3)
+        finish(6)
+        q_units(7)
+        finish(7, True)

@@ -21,8 +21,6 @@ UNITS = B * J // BU
 FLOPS = 2 * B * T * DM * 3 * H
 
 MK, MV, MQ = 0, 1, 2
-S_PERM = ()
-G_ADD = ()
 
 
 def tile_aftattention_t_kernel(tc, x, Wq, bq, Wk, bk, Wv, bv, wbias, out):
@@ -58,35 +56,37 @@ def tile_aftattention_t_kernel(tc, x, Wq, bq, Wk, bk, Wv, bv, wbias, out):
         e_tiles = {}
         p_tiles = {}
         n_sum = {}
+        sum_t = {}
         hw = {}
         th_tiles = {}
 
         def load_w(m):
             w_raw[m] = stage.tile([P, HB, DM], BF16, name="w_raw", tag="six", bufs=5, align_bytes=64)
-            for r in range(HB):
-                nc.sync.dma_start(out=w_raw[m][:, r, :], in_=w_dram[m][r * P : (r + 1) * P, :])
+            nc.sync.dma_start(out=w_raw[m][:], in_=w_dram[m].rearrange("(r p) k -> p r k", p=P))
 
         def batches(u):
             return slice(BU * (u % 2), BU * (u % 2) + BU)
 
-        def load_x(u):
+        def load_x(u, parts=(2, 2)):
             x_raw[u] = stage.tile([P, BU, DM], BF16, name="x_raw", tag="x_raw", bufs=4)
             src = x[batches(u)].rearrange("b (p j) k -> p j b k", j=J)[:, u // 2]
-            for k in range(0, BU, 2):
-                nc.sync.dma_start(out=x_raw[u][:, k : k + 2, :], in_=src[:, k : k + 2, :])
+            k = 0
+            for n in parts:
+                nc.sync.dma_start(out=x_raw[u][:, k : k + n, :], in_=src[:, k : k + n, :])
+                k += n
 
-        def permute_x(u):
-            for k in range(2):
-                x_perm[(u, k)] = stage.tile([P, 2 * DM // 2], F32, name="x_perm", tag="x_perm", bufs=3)
-                (nc.scalar.copy if u in S_PERM else nc.vector.tensor_copy)(
-                    out=x_perm[(u, k)][:].rearrange("p (jg u w) -> p jg u w", jg=4, u=2),
-                    in_=x_raw[u][:, 2 * k : 2 * k + 2, :]
-                    .rearrange("p j k -> p (j k)")
-                    .bitcast(F32)
-                    .rearrange("p (jg w u) -> p jg u w", jg=4, u=2),
-                )
+        def permute_x(u, k, engine):
+            copy = nc.scalar.copy if engine == "s" else nc.vector.tensor_copy
+            x_perm[(u, k)] = stage.tile([P, DM], F32, name="x_perm", tag="x_perm", bufs=2)
+            copy(
+                out=x_perm[(u, k)][:].rearrange("p (rg u w) -> p rg u w", rg=4, u=2),
+                in_=x_raw[u][:, 2 * k : 2 * k + 2, :]
+                .rearrange("p r k -> p (r k)")
+                .bitcast(F32)
+                .rearrange("p (rg w u) -> p rg u w", rg=4, u=2),
+            )
 
-        def transpose_words(dst_bank, words, permuted):
+        def transpose_words(dst_bank, words, permuted=False):
             for c in range(4):
                 g, u = c // 2, c % 2
                 src = words[:, c * P : (c + 1) * P] if permuted else words[:, 256 * g + u : 256 * (g + 1) : 2]
@@ -101,7 +101,7 @@ def tile_aftattention_t_kernel(tc, x, Wq, bq, Wk, bk, Wv, bv, wbias, out):
                 w_grp[m] = stage.tile([P, 2 * H * 4], BF16, name="w_grp", tag="six", bufs=5, align_bytes=64)
             grp32 = w_grp[m][:].bitcast(F32).rearrange("p (g h u) -> p g h u", g=2, u=2)
             ps = bank()
-            transpose_words(ps, w_raw[m][:, r, :].bitcast(F32), False)
+            transpose_words(ps, w_raw[m][:, r, :].bitcast(F32))
             copy_grouped(engine, grp32[:, :, r * P : (r + 1) * P, :], ps)
 
         def quantise_w(m, r):
@@ -118,10 +118,10 @@ def tile_aftattention_t_kernel(tc, x, Wq, bq, Wk, bk, Wv, bv, wbias, out):
             grp32 = x_grp[u][:].bitcast(F32).rearrange("p (g c u) -> p g c u", g=2, u=2)
             for c in range(BU):
                 ps = bank()
-                if (u, 0) in x_perm:
-                    transpose_words(ps, x_perm[(u, c // 2)][:, (c % 2) * 512 : (c % 2 + 1) * 512], True)
+                if (u, c // 2) in x_perm:
+                    transpose_words(ps, x_perm[(u, c // 2)][:, (c % 2) * DM // 2 : (c % 2 + 1) * DM // 2], True)
                 else:
-                    transpose_words(ps, x_raw[u][:, c, :].bitcast(F32), False)
+                    transpose_words(ps, x_raw[u][:, c, :].bitcast(F32))
                 copy_grouped(engines[c], grp32[:, :, c * P : (c + 1) * P, :], ps)
 
         def quantise_x(u, parts=1):
@@ -168,24 +168,46 @@ def tile_aftattention_t_kernel(tc, x, Wq, bq, Wk, bk, Wv, bv, wbias, out):
                     op1=ALU.mult,
                 )
 
-        def batch_sum(engine, dst, a, b, t):
+        def halve_by_block(dst, t):
             for hb in range(HB):
-                engine.tensor_tensor(out=t[:, hb, :], in0=a[:, hb, :], in1=b[:, hb, :], op=ALU.add)
-            for hb in range(HB):
-                engine.tensor_tensor(
+                nc.vector.tensor_tensor(
                     out=t[:, hb, 0 : N // 2], in0=t[:, hb, 0 : N // 2], in1=t[:, hb, N // 2 : N], op=ALU.add
                 )
             for hb in range(HB):
-                engine.tensor_tensor(out=dst[:, hb, :], in0=t[:, hb, 0:P], in1=t[:, hb, P : 2 * P], op=ALU.add)
+                nc.vector.tensor_tensor(out=dst[:, hb, :], in0=t[:, hb, 0:P], in1=t[:, hb, P : 2 * P], op=ALU.add)
 
         def sum_exponentials(j):
             t = stage.tile([P, HB, N], F32, name="sum_t", tag="sum_t", bufs=2)
-            batch_sum(nc.gpsimd if j in G_ADD else nc.vector, d_sum[:, j, :, :], e_tiles[2 * j], e_tiles[2 * j + 1], t)
+            for hb in range(HB):
+                nc.vector.tensor_tensor(
+                    out=t[:, hb, :], in0=e_tiles[2 * j][:, hb, :], in1=e_tiles[2 * j + 1][:, hb, :], op=ALU.add
+                )
+            halve_by_block(d_sum[:, j, :, :], t)
+
+        def start_product_sum(j):
+            sum_t[j] = stage.tile([P, HB, N], F32, name="sum_t", tag="sum_t", bufs=2)
+            n_sum[j] = stage.tile([P, HB, P], F32, name="n_sum", tag="n_sum", bufs=3)
+            nc.vector.tensor_tensor(out=sum_t[j][:], in0=p_tiles[2 * j][:], in1=p_tiles[2 * j + 1][:], op=ALU.add)
+
+        def finish_product_sums(js):
+            for j in js:
+                t = sum_t[j]
+                nc.vector.tensor_tensor(
+                    out=t[:, :, 0 : N // 2], in0=t[:, :, 0 : N // 2], in1=t[:, :, N // 2 : N], op=ALU.add
+                )
+            for j in js:
+                nc.vector.tensor_tensor(
+                    out=n_sum[j][:], in0=sum_t[j][:, :, 0:P], in1=sum_t[j][:, :, P : 2 * P], op=ALU.add
+                )
 
         def sum_products(j):
             t = stage.tile([P, HB, N], F32, name="sum_t", tag="sum_t", bufs=2)
             n_sum[j] = stage.tile([P, HB, P], F32, name="n_sum", tag="n_sum", bufs=3)
-            batch_sum(nc.vector, n_sum[j][:], p_tiles[2 * j], p_tiles[2 * j + 1], t)
+            for hb in range(HB):
+                nc.vector.tensor_tensor(
+                    out=t[:, hb, :], in0=p_tiles[2 * j][:, hb, :], in1=p_tiles[2 * j + 1][:, hb, :], op=ALU.add
+                )
+            halve_by_block(n_sum[j], t)
 
         def reciprocal(j0, j1):
             d = d_sum[:, j0:j1, :, :]
@@ -218,16 +240,19 @@ def tile_aftattention_t_kernel(tc, x, Wq, bq, Wk, bk, Wv, bv, wbias, out):
                 for c in range(BU):
                     nc.tensor.transpose(ps[:, c * P : (c + 1) * P], th_tiles[(u, hb)][:, c * P : (c + 1) * P], ident[:])
                 cols = slice(hb * P, (hb + 1) * P)
-                nc.vector.scalar_tensor_tensor(
-                    out=o_sb[:, :, cols],
-                    in0=ps[:].rearrange("p (c h) -> p c h", c=BU),
-                    scalar=1.0,
-                    in1=hw[u // 2][:, cols].unsqueeze(1).to_broadcast([P, BU, P]),
-                    op0=ALU.add,
-                    op1=ALU.mult,
-                )
-                if fine:
-                    nc.sync.dma_start(out=dst[:, :, cols], in_=o_sb[:, :, cols])
+                step = BU // 2 if fine and hb == HB - 1 else BU
+                for b in range(0, BU, step):
+                    rows = slice(b, b + step)
+                    nc.vector.scalar_tensor_tensor(
+                        out=o_sb[:, rows, cols],
+                        in0=ps[:].rearrange("p (c h) -> p c h", c=BU)[:, rows, :],
+                        scalar=1.0,
+                        in1=hw[u // 2][:, cols].unsqueeze(1).to_broadcast([P, step, P]),
+                        op0=ALU.add,
+                        op1=ALU.mult,
+                    )
+                    if fine:
+                        nc.sync.dma_start(out=dst[:, rows, cols], in_=o_sb[:, rows, cols])
             if not fine:
                 nc.sync.dma_start(out=dst, in_=o_sb[:])
 
@@ -246,13 +271,13 @@ def tile_aftattention_t_kernel(tc, x, Wq, bq, Wk, bk, Wv, bv, wbias, out):
         nc.vector.memset(warm[:], 0.0)
         nc.scalar.activation(out=warm[:], in_=warm[:], func=ACT.Exp)
 
-        load_x(0)
+        load_x(0, (1, 1, 2))
         load_w(MK)
         load_x(1)
+        load_w(MV)
         load_x(2)
         load_x(3)
-        load_w(MV)
-        transpose_x(0, "svvs")
+        transpose_x(0, "ssvs")
         load_x(4)
         transpose_w(MK, 0, "s")
         quantise_x(0, 2)
@@ -260,59 +285,64 @@ def tile_aftattention_t_kernel(tc, x, Wq, bq, Wk, bk, Wv, bv, wbias, out):
         transpose_w(MK, 2, "s")
         quantise_w(MK, 0)
         quantise_w(MK, 1)
-        transpose_x(1, "sssv")
+        transpose_x(1, "vsvs")
         load_x(5)
         quantise_w(MK, 2)
-        bias_rows()
         quantise_x(1)
-        transpose_x(2, "svsv")
-        load_x(6)
-        transpose_x(3, "svsv")
-        load_x(7)
-        quantise_x(2)
-        bias_columns()
+        bias_rows()
         transpose_w(MV, 0, "s")
-        transpose_w(MV, 1, "v")
+        transpose_w(MV, 1, "s")
         transpose_w(MV, 2, "s")
-        quantise_x(3)
-        k_units(0)
-        k_units(1)
+        permute_x(2, 0, "v")
         quantise_w(MV, 0)
+        k_units(0)
+        permute_x(2, 1, "v")
         quantise_w(MV, 1)
         quantise_w(MV, 2)
-        sum_exponentials(0)
-        k_units(2)
-        k_units(3)
-        sum_exponentials(1)
-        reciprocal(0, 2)
+        transpose_x(2, "svss")
+        load_x(6)
+        bias_columns()
+        permute_x(3, 0, "v")
         v_units(0)
+        permute_x(3, 1, "s")
+        quantise_x(2)
+        k_units(1)
+        sum_exponentials(0)
+        transpose_x(3)
+        load_x(7)
+        k_units(2)
+        quantise_x(3)
         v_units(1)
-        v_units(2)
-        v_units(3)
+        sum_products(0)
+        permute_x(4, 0, "s")
+        k_units(3)
         load_w(MQ)
         transpose_x(4)
-        sum_products(0)
+        sum_exponentials(1)
         transpose_x(5)
         quantise_x(4)
+        reciprocal(0, 2)
+        v_units(2)
+        v_units(3)
+        quantise_x(5)
         transpose_w(MQ, 0, "s")
         transpose_w(MQ, 1, "s")
         transpose_w(MQ, 2, "s")
-        quantise_x(5)
         sum_products(1)
         quantise_w(MQ, 0)
-        mean_product(0)
-        mean_product(1)
         transpose_x(6)
         k_units(4)
         k_units(5)
         quantise_w(MQ, 1)
         quantise_w(MQ, 2)
+        mean_product(0)
+        mean_product(1)
+        quantise_x(6)
         v_units(4)
         q_units(0)
         mean_transpose(0)
         mean_transpose(1)
         transpose_x(7)
-        quantise_x(6)
         sum_exponentials(2)
         finish(0)
         v_units(5)

from contextlib import ExitStack

import concourse.masks as masks
import concourse.mybir as mybir

F32 = mybir.dt.float32
BF16 = mybir.dt.bfloat16
U32 = mybir.dt.uint32
U8 = mybir.dt.uint8
FP8X4 = mybir.dt.float8_e4m3fn_x4
ACT = mybir.ActivationFunctionType
ALU = mybir.AluOpType

B, T, DM, H = 8, 512, 1024, 384
P = 128
J = T // P
HB = H // P
BU = 4
N = BU * P
UNITS = B * J // BU
FLOPS = 2 * B * T * DM * 3 * H

MK, MV, MQ = 0, 1, 2


def tile_aftattention_t_kernel(tc, x, Wq, bq, Wk, bk, Wv, bv, wbias, out):
    nc = tc.nc
    with ExitStack() as ctx:
        keep = ctx.enter_context(tc.tile_pool(name="keep", bufs=1))
        stage = ctx.enter_context(tc.tile_pool(name="stage", bufs=2))
        psum = ctx.enter_context(tc.psum_pool(name="psum", bufs=8))
        ctx.enter_context(tc.manual_schedule())

        def bank():
            return psum.tile([P, N], F32, name="ps", tag="ps", bufs=8)

        ident = keep.tile([P, P], F32, name="ident")
        masks.make_identity(nc, ident[:])

        w_codes = keep.tile([P, 3, 2 * H], U32, name="w_codes", align_bytes=64)
        w_sc = keep.tile([P, 3, 2 * H], U8, name="w_sc", align_bytes=64)
        x_codes = keep.tile([P, UNITS, 2, N], U32, name="x_codes", align_bytes=64)
        x_sc = keep.tile([P, UNITS, 2, N], U8, name="x_sc", align_bytes=64)
        b_rows = keep.tile([P, P], BF16, name="b_rows")
        b_rows32 = keep.tile([P, P], F32, name="b_rows32")
        b_cols = keep.tile([P, 8], F32, name="b_cols")
        warm = keep.tile([P, 1], F32, name="warm")
        d_sum = keep.tile([P, J, HB, P], F32, name="d_sum")

        w_dram = (Wk, Wv, Wq)
        w_raw = {}
        w_grp = {}
        x_raw = {}
        x_perm = {}
        x_grp = {}
        e_tiles = {}
        p_tiles = {}
        n_sum = {}
        sum_t = {}
        hw = {}
        th_tiles = {}

        def load_w(m):
            w_raw[m] = stage.tile([P, HB, DM], BF16, name="w_raw", tag="six", bufs=5, align_bytes=64)
            nc.sync.dma_start(out=w_raw[m][:], in_=w_dram[m].rearrange("(r p) k -> p r k", p=P))

        def batches(u):
            return slice(BU * (u % 2), BU * (u % 2) + BU)

        def load_x(u, parts=(2, 2)):
            x_raw[u] = stage.tile([P, BU, DM], BF16, name="x_raw", tag="x_raw", bufs=4)
            src = x[batches(u)].rearrange("b (p j) k -> p j b k", j=J)[:, u // 2]
            k = 0
            for n in parts:
                nc.sync.dma_start(out=x_raw[u][:, k : k + n, :], in_=src[:, k : k + n, :])
                k += n

        def permute_x(u, k, engine):
            copy = nc.scalar.copy if engine == "s" else nc.vector.tensor_copy
            x_perm[(u, k)] = stage.tile([P, DM], F32, name="x_perm", tag="x_perm", bufs=2)
            copy(
                out=x_perm[(u, k)][:].rearrange("p (rg u w) -> p rg u w", rg=4, u=2),
                in_=x_raw[u][:, 2 * k : 2 * k + 2, :]
                .rearrange("p r k -> p (r k)")
                .bitcast(F32)
                .rearrange("p (rg w u) -> p rg u w", rg=4, u=2),
            )

        def transpose_words(dst_bank, words, permuted=False):
            for c in range(4):
                g, u = c // 2, c % 2
                src = words[:, c * P : (c + 1) * P] if permuted else words[:, 256 * g + u : 256 * (g + 1) : 2]
                nc.tensor.transpose(dst_bank[:, c * P : (c + 1) * P], src, ident[:])

        def copy_grouped(engine, dst, ps):
            copy = nc.scalar.copy if engine == "s" else nc.vector.tensor_copy
            copy(out=dst, in_=ps[:].rearrange("p (g u r) -> p g r u", g=2, u=2))

        def transpose_w(m, r, engine):
            if r == 0:
                w_grp[m] = stage.tile([P, 2 * H * 4], BF16, name="w_grp", tag="six", bufs=5, align_bytes=64)
            grp32 = w_grp[m][:].bitcast(F32).rearrange("p (g h u) -> p g h u", g=2, u=2)
            ps = bank()
            transpose_words(ps, w_raw[m][:, r, :].bitcast(F32))
            copy_grouped(engine, grp32[:, :, r * P : (r + 1) * P, :], ps)

        def quantise_w(m, r):
            for g in range(2):
                cols = slice(g * H + r * P, g * H + (r + 1) * P)
                nc.vector.quantize_mx(
                    out=w_codes[:, m, cols].bitcast(FP8X4),
                    scales=w_sc[:, m, cols],
                    in_=w_grp[m][:, 4 * (g * H + r * P) : 4 * (g * H + (r + 1) * P)],
                )

        def transpose_x(u, engines="ssss"):
            x_grp[u] = stage.tile([P, 2 * N * 4], BF16, name="x_grp", tag="x_grp", bufs=2, align_bytes=64)
            grp32 = x_grp[u][:].bitcast(F32).rearrange("p (g c u) -> p g c u", g=2, u=2)
            for c in range(BU):
                ps = bank()
                if (u, c // 2) in x_perm:
                    transpose_words(ps, x_perm[(u, c // 2)][:, (c % 2) * DM // 2 : (c % 2 + 1) * DM // 2], True)
                else:
                    transpose_words(ps, x_raw[u][:, c, :].bitcast(F32))
                copy_grouped(engines[c], grp32[:, :, c * P : (c + 1) * P, :], ps)

        def quantise_x(u, parts=1):
            for c in range(parts):
                w = N // parts
                for g in range(2):
                    nc.vector.quantize_mx(
                        out=x_codes[:, u, g, c * w : (c + 1) * w].bitcast(FP8X4),
                        scales=x_sc[:, u, g, c * w : (c + 1) * w],
                        in_=x_grp[u][:, 4 * (g * N + c * w) : 4 * (g * N + (c + 1) * w)],
                    )

        def project(m, u, hb):
            ps = bank()
            for g in range(2):
                cols = slice(g * H + hb * P, g * H + (hb + 1) * P)
                nc.tensor.matmul_mx(
                    out=ps[:],
                    lhsT=w_codes[:, m, cols].bitcast(FP8X4),
                    lhsT_scale=w_sc[:, m, cols],
                    rhs=x_codes[:, u, g, :].bitcast(FP8X4),
                    rhs_scale=x_sc[:, u, g, :],
                    start=(g == 0),
                    stop=(g == 1),
                )
            return ps

        def k_units(u):
            e_tiles[u] = stage.tile([P, HB, N], F32, name="e_t", tag="e_t", bufs=4)
            for hb in range(HB):
                ps = project(MK, u, hb)
                nc.scalar.activation(out=e_tiles[u][:, hb, :], in_=ps[:], func=ACT.Exp)

        def v_units(u):
            p_tiles[u] = stage.tile([P, HB, N], F32, name="p_t", tag="six", bufs=5, align_bytes=64)
            for hb in range(HB):
                ps = project(MV, u, hb)
                nc.vector.scalar_tensor_tensor(
                    out=p_tiles[u][:, hb, :],
                    in0=ps[:],
                    scalar=b_cols[:, HB + hb : HB + hb + 1],
                    in1=e_tiles[u][:, hb, :],
                    op0=ALU.add,
                    op1=ALU.mult,
                )

        def halve_by_block(dst, t):
            for hb in range(HB):
                nc.vector.tensor_tensor(
                    out=t[:, hb, 0 : N // 2], in0=t[:, hb, 0 : N // 2], in1=t[:, hb, N // 2 : N], op=ALU.add
                )
            for hb in range(HB):
                nc.vector.tensor_tensor(out=dst[:, hb, :], in0=t[:, hb, 0:P], in1=t[:, hb, P : 2 * P], op=ALU.add)

        def sum_exponentials(j):
            t = stage.tile([P, HB, N], F32, name="sum_t", tag="sum_t", bufs=2)
            for hb in range(HB):
                nc.vector.tensor_tensor(
                    out=t[:, hb, :], in0=e_tiles[2 * j][:, hb, :], in1=e_tiles[2 * j + 1][:, hb, :], op=ALU.add
                )
            halve_by_block(d_sum[:, j, :, :], t)

        def start_product_sum(j):
            sum_t[j] = stage.tile([P, HB, N], F32, name="sum_t", tag="sum_t", bufs=2)
            n_sum[j] = stage.tile([P, HB, P], F32, name="n_sum", tag="n_sum", bufs=3)
            nc.vector.tensor_tensor(out=sum_t[j][:], in0=p_tiles[2 * j][:], in1=p_tiles[2 * j + 1][:], op=ALU.add)

        def finish_product_sums(js):
            for j in js:
                t = sum_t[j]
                nc.vector.tensor_tensor(
                    out=t[:, :, 0 : N // 2], in0=t[:, :, 0 : N // 2], in1=t[:, :, N // 2 : N], op=ALU.add
                )
            for j in js:
                nc.vector.tensor_tensor(
                    out=n_sum[j][:], in0=sum_t[j][:, :, 0:P], in1=sum_t[j][:, :, P : 2 * P], op=ALU.add
                )

        def sum_products(j):
            t = stage.tile([P, HB, N], F32, name="sum_t", tag="sum_t", bufs=2)
            n_sum[j] = stage.tile([P, HB, P], F32, name="n_sum", tag="n_sum", bufs=3)
            for hb in range(HB):
                nc.vector.tensor_tensor(
                    out=t[:, hb, :], in0=p_tiles[2 * j][:, hb, :], in1=p_tiles[2 * j + 1][:, hb, :], op=ALU.add
                )
            halve_by_block(n_sum[j], t)

        def reciprocal(j0, j1):
            d = d_sum[:, j0:j1, :, :]
            nc.scalar.activation(out=d, in_=d, func=ACT.Ln)
            nc.scalar.activation(out=d, in_=d, func=ACT.Exp, scale=-1.0)

        def mean_product(j):
            nc.vector.tensor_tensor(out=n_sum[j][:], in0=n_sum[j][:], in1=d_sum[:, j, :, :], op=ALU.mult)

        def mean_transpose(j):
            hw[j] = stage.tile([P, H], F32, name="hw", tag="hw", bufs=3)
            ps = bank()
            for hb in range(HB):
                nc.tensor.transpose(ps[:, hb * P : (hb + 1) * P], n_sum[j][:, hb, :], ident[:])
            nc.scalar.mul(out=hw[j][:], in_=ps[:, 0:H], mul=0.5)

        def q_units(u):
            for hb in range(HB):
                th_tiles[(u, hb)] = stage.tile([P, N], F32, name="th", tag="th", bufs=12)
                ps = project(MQ, u, hb)
                nc.scalar.activation(
                    out=th_tiles[(u, hb)][:], in_=ps[:], func=ACT.Tanh, bias=b_cols[:, hb : hb + 1], scale=0.5
                )

        def finish(u, fine=False):
            o_sb = stage.tile([P, BU, H], F32, name="o_sb", tag="o_sb", bufs=3)
            dst = out[batches(u)].rearrange("b (p j) h -> p j b h", j=J)[:, u // 2]
            for hb in range(HB):
                ps = bank()
                for c in range(BU):
                    nc.tensor.transpose(ps[:, c * P : (c + 1) * P], th_tiles[(u, hb)][:, c * P : (c + 1) * P], ident[:])
                cols = slice(hb * P, (hb + 1) * P)
                step = BU // 2 if fine and hb == HB - 1 else BU
                for b in range(0, BU, step):
                    rows = slice(b, b + step)
                    nc.vector.scalar_tensor_tensor(
                        out=o_sb[:, rows, cols],
                        in0=ps[:].rearrange("p (c h) -> p c h", c=BU)[:, rows, :],
                        scalar=1.0,
                        in1=hw[u // 2][:, cols].unsqueeze(1).to_broadcast([P, step, P]),
                        op0=ALU.add,
                        op1=ALU.mult,
                    )
                    if fine:
                        nc.sync.dma_start(out=dst[:, rows, cols], in_=o_sb[:, rows, cols])
            if not fine:
                nc.sync.dma_start(out=dst, in_=o_sb[:])

        def bias_rows():
            nc.vector.tensor_copy(out=b_rows32[:], in_=b_rows[:])

        def bias_columns():
            ps = bank()
            nc.tensor.transpose(ps[:, 0:P], b_rows32[:], ident[:])
            nc.vector.tensor_scalar_mul(out=b_cols[:, 0:HB], in0=ps[:, 0:HB], scalar1=0.5)
            nc.vector.tensor_copy(out=b_cols[:, HB : 2 * HB], in_=ps[:, HB : 2 * HB])

        nc.vector.memset(b_rows[:], 0.0)
        nc.scalar.dma_start(out=b_rows[0:HB, :], in_=bq.rearrange("(r c) -> r c", c=P))
        nc.scalar.dma_start(out=b_rows[HB : 2 * HB, :], in_=bv.rearrange("(r c) -> r c", c=P))
        nc.vector.memset(warm[:], 0.0)
        nc.scalar.activation(out=warm[:], in_=warm[:], func=ACT.Exp)

        load_x(0, (1, 1, 2))
        load_w(MK)
        load_x(1)
        load_w(MV)
        load_x(2)
        load_x(3)
        transpose_x(0, "ssvs")
        load_x(4)
        transpose_w(MK, 0, "s")
        quantise_x(0, 2)
        transpose_w(MK, 1, "v")
        transpose_w(MK, 2, "s")
        quantise_w(MK, 0)
        quantise_w(MK, 1)
        transpose_x(1, "vsvs")
        load_x(5)
        quantise_w(MK, 2)
        quantise_x(1)
        bias_rows()
        transpose_w(MV, 0, "s")
        transpose_w(MV, 1, "s")
        transpose_w(MV, 2, "s")
        permute_x(2, 0, "v")
        quantise_w(MV, 0)
        k_units(0)
        permute_x(2, 1, "v")
        quantise_w(MV, 1)
        quantise_w(MV, 2)
        transpose_x(2, "svss")
        load_x(6)
        bias_columns()
        permute_x(3, 0, "v")
        v_units(0)
        permute_x(3, 1, "s")
        quantise_x(2)
        k_units(1)
        sum_exponentials(0)
        transpose_x(3)
        load_x(7)
        k_units(2)
        quantise_x(3)
        v_units(1)
        sum_products(0)
        permute_x(4, 0, "s")
        k_units(3)
        load_w(MQ)
        transpose_x(4)
        sum_exponentials(1)
        transpose_x(5)
        quantise_x(4)
        reciprocal(0, 2)
        v_units(2)
        v_units(3)
        quantise_x(5)
        transpose_w(MQ, 0, "s")
        transpose_w(MQ, 1, "s")
        transpose_w(MQ, 2, "s")
        sum_products(1)
        quantise_w(MQ, 0)
        transpose_x(6)
        k_units(4)
        k_units(5)
        quantise_w(MQ, 1)
        quantise_w(MQ, 2)
        mean_product(0)
        mean_product(1)
        quantise_x(6)
        v_units(4)
        q_units(0)
        mean_transpose(0)
        mean_transpose(1)
        transpose_x(7)
        sum_exponentials(2)
        finish(0)
        v_units(5)
        reciprocal(2, 3)
        k_units(6)
        q_units(1)
        quantise_x(7)
        k_units(7)
        sum_products(2)
        v_units(6)
        mean_product(2)
        q_units(2)
        q_units(3)
        mean_transpose(2)
        sum_exponentials(3)
        finish(1)
        finish(2)
        finish(3)
        reciprocal(3, 4)
        v_units(7)
        q_units(4)
        sum_products(3)
        q_units(5)
        finish(4)
        q_units(6)
        mean_product(3)
        finish(5)
        mean_transpose(3)
        finish(6)
        q_units(7)
        finish(7, True)
